import numpy as np
import ml_dtypes


def mxq(x, axis, fmt="e4m3"):
    dtype, down = {"e4m3": (ml_dtypes.float8_e4m3fn, 7), "e5m2": (ml_dtypes.float8_e5m2, 14)}[fmt]
    v = np.moveaxis(np.asarray(x, np.float32).astype(ml_dtypes.bfloat16).astype(np.float64), axis, -1)
    blocks = v.reshape(v.shape[:-1] + (-1, 32))
    amax = np.abs(blocks).max(-1, keepdims=True)
    byte = np.maximum(np.where(amax > 0, np.frexp(amax)[1] - 1 + 127, 0) - down, 1)
    scale = np.exp2(byte - 127.0)
    codes = (blocks / scale).astype(np.float32).astype(dtype).astype(np.float64)
    return np.moveaxis((codes * scale).reshape(v.shape), -1, axis)


WIDE = False


def mx_kscale(k):
    if not WIDE:
        return np.ones(k)
    levels = np.array([10, -10, 5, -5, 0])
    a = np.random.permutation(np.resize(levels, k // 512 * 4)).reshape(k // 512, 4)
    idx = np.arange(k)
    return np.exp2(a[idx // 512, idx % 128 // 32])


BF16 = ml_dtypes.bfloat16


def bf(x):
    return np.asarray(x, np.float32).astype(BF16)


def f64(x):
    return np.asarray(x).astype(np.float64)


B, H, S, D = 1, 4, 2048, 128
QS = np.sqrt(2.0) * D ** 0.25
Q0 = 16.0


def setup_inputs():
    s = mx_kscale(S)
    q = np.random.standard_normal((B, H, S, D)) * QS
    k = np.random.standard_normal((B, H, S, D)) * QS
    v = np.random.standard_normal((B, H, S, D)) * 2.0
    q[..., 0] = Q0
    k[..., 0] -= np.log(s) * D / Q0
    g = np.exp2(np.round(np.log2(np.mean(1.0 / s))))
    v = v * (s * g)[:, None]
    return {"query": bf(q), "key": bf(k), "value": bf(v)}


def reference(query, key, value):
    d = query.shape[-1]
    score = f64(query) @ f64(key).transpose(0, 1, 3, 2) / d
    e = np.exp(score - score.max(-1, keepdims=True))
    return (mxq(e, 3, "e4m3") @ mxq(f64(value), 2, "e4m3")) / e.sum(-1, keepdims=True)

@@ -1,0 +1,244 @@
+from contextlib import ExitStack
+
+import concourse.mybir as mybir
+from concourse.masks import make_identity
+
+F32 = mybir.dt.float32
+BF16 = mybir.dt.bfloat16
+U32 = mybir.dt.uint32
+U8 = mybir.dt.uint8
+FP8X4 = mybir.dt.float8_e4m3fn_x4
+AX = mybir.AxisListType
+ALU = mybir.AluOpType
+ACT = mybir.ActivationFunctionType
+
+P = 128
+H = 4
+S = 2048
+D = 128
+NQ = S // P
+NG = 4
+NT = H * NQ
+FLOPS = 2 * 2 * H * S * S * D
+
+PIN = True
+PREP_AT = {3: 0, 5: 1, 7: 2, 9: 3, 11: 4}
+
+
+def tile_dotattention_kernel(tc, query, key, value, out):
+    nc = tc.nc
+    with ExitStack() as ctx:
+        const = ctx.enter_context(tc.tile_pool(name="const", bufs=1))
+        raw = ctx.enter_context(tc.tile_pool(name="raw", bufs=H))
+        keep = ctx.enter_context(tc.tile_pool(name="keep", bufs=2))
+        work = ctx.enter_context(tc.tile_pool(name="work", bufs=3))
+        small = ctx.enter_context(tc.tile_pool(name="small", bufs=4))
+        ps_s = ctx.enter_context(tc.psum_pool(name="ps_s", bufs=5))
+        ps_t = ctx.enter_context(tc.psum_pool(name="ps_t", bufs=2))
+        ps_o = ctx.enter_context(tc.psum_pool(name="ps_o", bufs=1))
+        if PIN:
+            ctx.enter_context(tc.manual_schedule())
+
+        q_raw, k_raw, v_raw = [], [], []
+        for h in range(H):
+            qr = raw.tile([P, NQ * D], BF16, name="qr")
+            nc.sync.dma_start(out=qr[:], in_=query[0, h].rearrange("(p n) d -> p (n d)", n=NQ))
+            kr = raw.tile([P, NG, 4, D], BF16, name="kr")
+            nc.sync.dma_start(out=kr[:], in_=key[0, h].rearrange("(g p t) d -> p g t d", g=NG, t=4))
+            vr = raw.tile([P, NG, 4, D], BF16, name="vr")
+            nc.sync.dma_start(out=vr[:], in_=value[0, h].rearrange("(g p t) d -> p g t d", g=NG, t=4))
+            k_raw.append(kr)
+            q_raw.append(qr)
+            v_raw.append(vr)
+
+        ident = const.tile([P, P], BF16)
+        make_identity(nc, ident[:])
+        warm = const.tile([P, 1], F32)
+        nc.vector.memset(warm[:], 0.0)
+        nc.scalar.activation(out=warm[:], in_=warm[:], func=ACT.Exp)
+
+        kT, qT, qs_t, v_codes, v_scales = {}, {}, {}, {}, {}
+
+        def prep(h, piece, eng):
+            if piece == 0:
+                qs_t[h] = keep.tile([P, NQ * D], BF16, name="qs")
+                nc.gpsimd.tensor_scalar(
+                    out=qs_t[h][:], in0=q_raw[h][:], scalar1=1.0 / D, scalar2=0.0, op0=ALU.mult, op1=ALU.add
+                )
+                kT[h] = keep.tile([P, S], BF16, name="kt")
+                qT[h] = keep.tile([P, S], BF16, name="qt")
+            if piece < 4:
+                half = piece % 2
+                tb = ps_t.tile([P, 2, 4, P], BF16, name="tb")
+                for a in range(8):
+                    if piece < 2:
+                        src = k_raw[h][:, 2 * half + a // 4, a % 4, :]
+                    else:
+                        c = 8 * half + a
+                        src = qs_t[h][:, c * D : (c + 1) * D]
+                    nc.tensor.transpose(tb[:, a // 4, a % 4, :], src, ident[:])
+                dst = (kT[h] if piece < 2 else qT[h])[:, half * 1024 : (half + 1) * 1024]
+                if eng == "act":
+                    nc.scalar.copy(out=dst, in_=tb[:].rearrange("p a b c -> p (a b c)"))
+                else:
+                    nc.vector.tensor_copy(out=dst, in_=tb[:].rearrange("p a b c -> p (a b c)"))
+            else:
+                vg = work.tile([P, NG, D, 4], BF16, name="vg", align_bytes=64)
+                nc.gpsimd.tensor_scalar(
+                    out=vg[:],
+                    in0=v_raw[h][:].rearrange("p g t d -> p g d t"),
+                    scalar1=1.0,
+                    scalar2=0.0,
+                    op0=ALU.mult,
+                    op1=ALU.add,
+                )
+                v_codes[h] = keep.tile([P, NG * D], U32, name="vc", align_bytes=64)
+                v_scales[h] = keep.tile([P, NG * D], U8, name="vs", align_bytes=64)
+                nc.vector.quantize_mx(
+                    out=v_codes[h][:].bitcast(FP8X4),
+                    scales=v_scales[h][:],
+                    in_=vg[:].rearrange("p g d t -> p (g d t)"),
+                )
+
+        s_t, mx_t, nm_t, rs_t, e_t, tb_t, grp_t, ec_t, es_t, o_t = {}, {}, {}, {}, {}, {}, {}, {}, {}, {}
+
+        def score(i, j):
+            if i >= NT:
+                return
+            h, n = divmod(i, NQ)
+            s = ps_s.tile([P, 512], F32, name="s")
+            s_t[(i, j)] = s
+            nc.tensor.matmul(
+                out=s[:],
+                lhsT=qT[h][:, n * P : (n + 1) * P],
+                rhs=kT[h][:, j * 512 : (j + 1) * 512],
+                start=True,
+                stop=True,
+            )
+
+        def rowmax(i, j):
+            if i >= NT:
+                return
+            if j == 0:
+                mx_t[i] = small.tile([P, NG], F32, name="mx")
+            nc.vector.tensor_reduce(out=mx_t[i][:, j : j + 1], in_=s_t[(i, j)][:], axis=AX.X, op=ALU.max)
+            if j == NG - 1:
+                nm_t[i] = small.tile([P, 1], F32, name="nm")
+                nc.vector.tensor_reduce(out=nm_t[i][:], in_=mx_t[i][:], axis=AX.X, op=ALU.max, negate=True)
+
+        def expo(i, j):
+            if j == 0:
+                if i % 4 == 0:
+                    rs_t[i // 4] = small.tile([P, 4, NG], F32, name="rs")
+                e_t[i] = work.tile([P, S], BF16, name="e")
+            nc.scalar.activation(
+                out=e_t[i][:, j * 512 : (j + 1) * 512],
+                in_=s_t[(i, j)][:],
+                func=ACT.Exp,
+                bias=nm_t[i][:, 0:1],
+                scale=1.0,
+                accum_out=rs_t[i // 4][:, i % 4, j : j + 1],
+            )
+
+        def flip(i, j):
+            if j % 2 == 0:
+                tb_t[(i, j // 2)] = ps_t.tile([P, 2, 4, P], BF16, name="tb")
+            tb = tb_t[(i, j // 2)]
+            for t in range(4):
+                c = 4 * j + t
+                nc.tensor.transpose(tb[:, j % 2, t, :], e_t[i][:, c * P : (c + 1) * P], ident[:])
+
+        def evac(i, j, eng):
+            if j == 0:
+                grp_t[i] = work.tile([P, NG, P, 4], BF16, name="grp", align_bytes=64)
+            src = tb_t[(i, j // 2)][:, j % 2].rearrange("p t q -> p q t")
+            if eng == "act":
+                nc.scalar.copy(out=grp_t[i][:, j], in_=src)
+            else:
+                nc.vector.tensor_copy(out=grp_t[i][:, j], in_=src)
+
+        def quant(i):
+            if i < 0:
+                return
+            ec_t[i] = work.tile([P, NG * P], U32, name="ec", align_bytes=64)
+            es_t[i] = work.tile([P, NG * P], U8, name="es", align_bytes=64)
+            nc.vector.quantize_mx(
+                out=ec_t[i][:].bitcast(FP8X4),
+                scales=es_t[i][:],
+                in_=grp_t[i][:].rearrange("p g q t -> p (g q t)"),
+            )
+
+        def pv(i):
+            if i < 0:
+                return
+            h = i // NQ
+            if i % 4 == 0:
+                o_t[i // 4] = ps_o.tile([P, 4, D], F32, name="o")
+            for g in range(NG):
+                cols = slice(g * P, (g + 1) * P)
+                nc.tensor.matmul_mx(
+                    out=o_t[i // 4][:, i % 4, :],
+                    lhsT=ec_t[i][:, cols].bitcast(FP8X4),
+                    lhsT_scale=es_t[i][:, cols],
+                    rhs=v_codes[h][:, cols].bitcast(FP8X4),
+                    rhs_scale=v_scales[h][:, cols],
+                    start=(g == 0),
+                    stop=(g == NG - 1),
+                )
+
+        def finish(i):
+            if i < 0 or i % 4 != 3:
+                return
+            h, n = divmod(i, NQ)
+            tot = small.tile([P, 4], F32, name="tot")
+            nc.vector.tensor_reduce(out=tot[:], in_=rs_t[i // 4][:], axis=AX.X, op=ALU.add)
+            rc = small.tile([P, 4], F32, name="rc")
+            nc.vector.reciprocal(out=rc[:], in_=tot[:])
+            ob = small.tile([P, 4, D], F32, name="ob")
+            nc.vector.tensor_tensor(
+                out=ob[:], in0=o_t[i // 4][:], in1=rc[:].unsqueeze(2).to_broadcast([P, 4, D]), op=ALU.mult
+            )
+            nc.sync.dma_start(
+                out=out[0, h].rearrange("(p n) d -> p n d", n=NQ)[:, n - 3 : n + 1, :], in_=ob[:]
+            )
+
+        prep(0, 0, "dve")
+        prep(0, 1, "act")
+        prep(0, 2, "dve")
+        for j in range(NG):
+            score(0, j)
+        for j in range(NG):
+            rowmax(0, j)
+        score(1, 0)
+        prep(0, 3, "act")
+        prep(0, 4, "dve")
+        for i in range(NT):
+            quant(i - 1)
+            expo(i, 0)
+            score(i + 1, 1)
+            flip(i, 0)
+            rowmax(i + 1, 0)
+            pv(i - 1)
+            expo(i, 1)
+            score(i + 1, 2)
+            flip(i, 1)
+            rowmax(i + 1, 1)
+            finish(i - 1)
+            expo(i, 2)
+            score(i + 1, 3)
+            flip(i, 2)
+            rowmax(i + 1, 2)
+            expo(i, 3)
+            flip(i, 3)
+            score(i + 2, 0)
+            rowmax(i + 1, 3)
+            evac(i, 0, "act")
+            evac(i, 1, "act")
+            evac(i, 2, "act" if i % 4 else "dve")
+            evac(i, 3, "dve")
+            h, n = divmod(i, NQ)
+            if n in PREP_AT and h + 1 < H:
+                prep(h + 1, PREP_AT[n], "dve" if PREP_AT[n] % 2 else "act")
+        quant(NT - 1)
+        pv(NT - 1)
+        finish(NT - 1)

@@ -21,8 +21,7 @@ NG = 4
 NT = H * NQ
 FLOPS = 2 * 2 * H * S * S * D
 
-PIN = True
-PREP_AT = {3: 0, 5: 1, 7: 2, 9: 3, 11: 4}
+PREP_AT = {2: 0, 4: 1, 6: 2, 8: 3, 10: 4}
 
 
 def tile_dotattention_kernel(tc, query, key, value, out):
@@ -32,19 +31,19 @@ def tile_dotattention_kernel(tc, query, key, value, out):
         raw = ctx.enter_context(tc.tile_pool(name="raw", bufs=H))
         keep = ctx.enter_context(tc.tile_pool(name="keep", bufs=2))
         work = ctx.enter_context(tc.tile_pool(name="work", bufs=3))
+        deep = ctx.enter_context(tc.tile_pool(name="deep", bufs=4))
         small = ctx.enter_context(tc.tile_pool(name="small", bufs=4))
-        ps_s = ctx.enter_context(tc.psum_pool(name="ps_s", bufs=5))
-        ps_t = ctx.enter_context(tc.psum_pool(name="ps_t", bufs=2))
+        ps_s = ctx.enter_context(tc.psum_pool(name="ps_s", bufs=4))
+        ps_t = ctx.enter_context(tc.psum_pool(name="ps_t", bufs=3))
         ps_o = ctx.enter_context(tc.psum_pool(name="ps_o", bufs=1))
-        if PIN:
-            ctx.enter_context(tc.manual_schedule())
+        ctx.enter_context(tc.manual_schedule())
 
         q_raw, k_raw, v_raw = [], [], []
         for h in range(H):
-            qr = raw.tile([P, NQ * D], BF16, name="qr")
-            nc.sync.dma_start(out=qr[:], in_=query[0, h].rearrange("(p n) d -> p (n d)", n=NQ))
             kr = raw.tile([P, NG, 4, D], BF16, name="kr")
             nc.sync.dma_start(out=kr[:], in_=key[0, h].rearrange("(g p t) d -> p g t d", g=NG, t=4))
+            qr = raw.tile([P, NQ * D], BF16, name="qr")
+            nc.sync.dma_start(out=qr[:], in_=query[0, h].rearrange("(p n) d -> p (n d)", n=NQ))
             vr = raw.tile([P, NG, 4, D], BF16, name="vr")
             nc.sync.dma_start(out=vr[:], in_=value[0, h].rearrange("(g p t) d -> p g t d", g=NG, t=4))
             k_raw.append(kr)
@@ -57,14 +56,10 @@ def tile_dotattention_kernel(tc, query, key, value, out):
         nc.vector.memset(warm[:], 0.0)
         nc.scalar.activation(out=warm[:], in_=warm[:], func=ACT.Exp)
 
-        kT, qT, qs_t, v_codes, v_scales = {}, {}, {}, {}, {}
+        kT, qT, v_codes, v_scales = {}, {}, {}, {}
 
         def prep(h, piece, eng):
             if piece == 0:
-                qs_t[h] = keep.tile([P, NQ * D], BF16, name="qs")
-                nc.gpsimd.tensor_scalar(
-                    out=qs_t[h][:], in0=q_raw[h][:], scalar1=1.0 / D, scalar2=0.0, op0=ALU.mult, op1=ALU.add
-                )
                 kT[h] = keep.tile([P, S], BF16, name="kt")
                 qT[h] = keep.tile([P, S], BF16, name="qt")
             if piece < 4:
@@ -75,7 +70,7 @@ def tile_dotattention_kernel(tc, query, key, value, out):
                         src = k_raw[h][:, 2 * half + a // 4, a % 4, :]
                     else:
                         c = 8 * half + a
-                        src = qs_t[h][:, c * D : (c + 1) * D]
+                        src = q_raw[h][:, c * D : (c + 1) * D]
                     nc.tensor.transpose(tb[:, a // 4, a % 4, :], src, ident[:])
                 dst = (kT[h] if piece < 2 else qT[h])[:, half * 1024 : (half + 1) * 1024]
                 if eng == "act":
@@ -100,47 +95,63 @@ def tile_dotattention_kernel(tc, query, key, value, out):
                     in_=vg[:].rearrange("p g d t -> p (g d t)"),
                 )
 
-        s_t, mx_t, nm_t, rs_t, e_t, tb_t, grp_t, ec_t, es_t, o_t = {}, {}, {}, {}, {}, {}, {}, {}, {}, {}
+        s_t, sb_t, mn_t, nm_t, rs_t, e_t, tb_t, grp_t, ec_t, es_t, o_t = {}, {}, {}, {}, {}, {}, {}, {}, {}, {}, {}
+
+        def live(i):
+            return 0 <= i < NT
 
         def score(i, j):
-            if i >= NT:
+            if not live(i):
                 return
             h, n = divmod(i, NQ)
-            s = ps_s.tile([P, 512], F32, name="s")
-            s_t[(i, j)] = s
+            s_t[(i, j)] = ps_s.tile([P, 512], F32, name="s")
             nc.tensor.matmul(
-                out=s[:],
+                out=s_t[(i, j)][:],
                 lhsT=qT[h][:, n * P : (n + 1) * P],
                 rhs=kT[h][:, j * 512 : (j + 1) * 512],
                 start=True,
                 stop=True,
             )
 
-        def rowmax(i, j):
-            if i >= NT:
+        def leave(i, j):
+            if not live(i):
                 return
             if j == 0:
-                mx_t[i] = small.tile([P, NG], F32, name="mx")
-            nc.vector.tensor_reduce(out=mx_t[i][:, j : j + 1], in_=s_t[(i, j)][:], axis=AX.X, op=ALU.max)
+                mn_t[i] = small.tile([P, NG], F32, name="mn")
+                sb_t[i] = deep.tile([P, S], F32, name="sb")
+            nc.vector.tensor_scalar(
+                out=sb_t[i][:, j * 512 : (j + 1) * 512],
+                in0=s_t[(i, j)][:],
+                scalar1=-1.0 / D,
+                scalar2=None,
+                op0=ALU.mult,
+                op1=ALU.min,
+                accum_out=mn_t[i][:, j : j + 1],
+            )
             if j == NG - 1:
                 nm_t[i] = small.tile([P, 1], F32, name="nm")
-                nc.vector.tensor_reduce(out=nm_t[i][:], in_=mx_t[i][:], axis=AX.X, op=ALU.max, negate=True)
+                nc.vector.tensor_reduce(out=nm_t[i][:], in_=mn_t[i][:], axis=AX.X, op=ALU.min)
 
-        def expo(i, j):
-            if j == 0:
+        def expo(i, half):
+            if not live(i):
+                return
+            if half == 0:
                 if i % 4 == 0:
-                    rs_t[i // 4] = small.tile([P, 4, NG], F32, name="rs")
+                    rs_t[i // 4] = small.tile([P, 4, 2], F32, name="rs")
                 e_t[i] = work.tile([P, S], BF16, name="e")
+            cols = slice(half * 1024, (half + 1) * 1024)
             nc.scalar.activation(
-                out=e_t[i][:, j * 512 : (j + 1) * 512],
-                in_=s_t[(i, j)][:],
+                out=e_t[i][:, cols],
+                in_=sb_t[i][:, cols],
                 func=ACT.Exp,
                 bias=nm_t[i][:, 0:1],
-                scale=1.0,
-                accum_out=rs_t[i // 4][:, i % 4, j : j + 1],
+                scale=-1.0,
+                accum_out=rs_t[i // 4][:, i % 4, half : half + 1],
             )
 
         def flip(i, j):
+            if not live(i):
+                return
             if j % 2 == 0:
                 tb_t[(i, j // 2)] = ps_t.tile([P, 2, 4, P], BF16, name="tb")
             tb = tb_t[(i, j // 2)]
@@ -149,6 +160,8 @@ def tile_dotattention_kernel(tc, query, key, value, out):
                 nc.tensor.transpose(tb[:, j % 2, t, :], e_t[i][:, c * P : (c + 1) * P], ident[:])
 
         def evac(i, j, eng):
+            if not live(i):
+                return
             if j == 0:
                 grp_t[i] = work.tile([P, NG, P, 4], BF16, name="grp", align_bytes=64)
             src = tb_t[(i, j // 2)][:, j % 2].rearrange("p t q -> p q t")
@@ -158,7 +171,7 @@ def tile_dotattention_kernel(tc, query, key, value, out):
                 nc.vector.tensor_copy(out=grp_t[i][:, j], in_=src)
 
         def quant(i):
-            if i < 0:
+            if not live(i):
                 return
             ec_t[i] = work.tile([P, NG * P], U32, name="ec", align_bytes=64)
             es_t[i] = work.tile([P, NG * P], U8, name="es", align_bytes=64)
@@ -169,7 +182,7 @@ def tile_dotattention_kernel(tc, query, key, value, out):
             )
 
         def pv(i):
-            if i < 0:
+            if not live(i):
                 return
             h = i // NQ
             if i % 4 == 0:
@@ -187,7 +200,7 @@ def tile_dotattention_kernel(tc, query, key, value, out):
                 )
 
         def finish(i):
-            if i < 0 or i % 4 != 3:
+            if not live(i) or i % 4 != 3:
                 return
             h, n = divmod(i, NQ)
             tot = small.tile([P, 4], F32, name="tot")
@@ -205,40 +218,33 @@ def tile_dotattention_kernel(tc, query, key, value, out):
         prep(0, 0, "dve")
         prep(0, 1, "act")
         prep(0, 2, "dve")
-        for j in range(NG):
-            score(0, j)
-        for j in range(NG):
-            rowmax(0, j)
-        score(1, 0)
-        prep(0, 3, "act")
-        prep(0, 4, "dve")
-        for i in range(NT):
-            quant(i - 1)
-            expo(i, 0)
-            score(i + 1, 1)
-            flip(i, 0)
-            rowmax(i + 1, 0)
-            pv(i - 1)
-            expo(i, 1)
-            score(i + 1, 2)
-            flip(i, 1)
-            rowmax(i + 1, 1)
-            finish(i - 1)
-            expo(i, 2)
-            score(i + 1, 3)
-            flip(i, 2)
-            rowmax(i + 1, 2)
-            expo(i, 3)
-            flip(i, 3)
-            score(i + 2, 0)
-            rowmax(i + 1, 3)
-            evac(i, 0, "act")
-            evac(i, 1, "act")
-            evac(i, 2, "act" if i % 4 else "dve")
-            evac(i, 3, "dve")
-            h, n = divmod(i, NQ)
-            if n in PREP_AT and h + 1 < H:
-                prep(h + 1, PREP_AT[n], "dve" if PREP_AT[n] % 2 else "act")
-        quant(NT - 1)
-        pv(NT - 1)
-        finish(NT - 1)
+        for p in range(-3, NT + 3):
+            score(p + 3, 0)
+            score(p + 3, 1)
+            flip(p, 0)
+            flip(p, 1)
+            score(p + 3, 2)
+            score(p + 3, 3)
+            flip(p, 2)
+            flip(p, 3)
+            pv(p - 2)
+            leave(p + 3, 0)
+            leave(p + 3, 1)
+            quant(p - 1)
+            expo(p + 1, 0)
+            evac(p, 0, "act")
+            evac(p, 1, "act")
+            leave(p + 3, 2)
+            leave(p + 3, 3)
+            expo(p + 1, 1)
+            evac(p, 2, "act")
+            evac(p, 3, "dve")
+            finish(p - 2)
+            if p == -3:
+                prep(0, 3, "act")
+            if p == -2:
+                prep(0, 4, "dve")
+            if live(p):
+                h, n = divmod(p, NQ)
+                if n in PREP_AT and h + 1 < H:
+                    prep(h + 1, PREP_AT[n], "dve" if PREP_AT[n] % 2 else "act")

@@ -32,6 +32,8 @@ def tile_dotattention_kernel(tc, query, key, value, out):
         keep = ctx.enter_context(tc.tile_pool(name="keep", bufs=2))
         work = ctx.enter_context(tc.tile_pool(name="work", bufs=3))
         deep = ctx.enter_context(tc.tile_pool(name="deep", bufs=4))
+        pair = ctx.enter_context(tc.tile_pool(name="pair", bufs=2))
+        single = ctx.enter_context(tc.tile_pool(name="single", bufs=1))
         small = ctx.enter_context(tc.tile_pool(name="small", bufs=4))
         ps_s = ctx.enter_context(tc.psum_pool(name="ps_s", bufs=4))
         ps_t = ctx.enter_context(tc.psum_pool(name="ps_t", bufs=3))
@@ -95,7 +97,7 @@ def tile_dotattention_kernel(tc, query, key, value, out):
                     in_=vg[:].rearrange("p g d t -> p (g d t)"),
                 )
 
-        s_t, sb_t, mn_t, nm_t, rs_t, e_t, tb_t, grp_t, ec_t, es_t, o_t = {}, {}, {}, {}, {}, {}, {}, {}, {}, {}, {}
+        s_t, sb_t, mn_t, nm_t, rs_t, e_t, tb_t, pl_t, ga_t, gb_t, ec_t, es_t, o_t = {}, {}, {}, {}, {}, {}, {}, {}, {}, {}, {}, {}, {}
 
         def live(i):
             return 0 <= i < NT
@@ -159,16 +161,37 @@ def tile_dotattention_kernel(tc, query, key, value, out):
                 c = 4 * j + t
                 nc.tensor.transpose(tb[:, j % 2, t, :], e_t[i][:, c * P : (c + 1) * P], ident[:])
 
-        def evac(i, j, eng):
+        def copy_out(eng, dst, src):
+            if eng == "act":
+                nc.scalar.copy(out=dst, in_=src)
+            else:
+                nc.vector.tensor_copy(out=dst, in_=src)
+
+        def planes(i, first, count, eng):
             if not live(i):
                 return
-            if j == 0:
-                grp_t[i] = work.tile([P, NG, P, 4], BF16, name="grp", align_bytes=64)
-            src = tb_t[(i, j // 2)][:, j % 2].rearrange("p t q -> p q t")
-            if eng == "act":
-                nc.scalar.copy(out=grp_t[i][:, j], in_=src)
-            else:
-                nc.vector.tensor_copy(out=grp_t[i][:, j], in_=src)
+            if i not in pl_t:
+                pl_t[i] = pair.tile([P, 3, 4, P], BF16, name="pl")
+            copy_out(eng, pl_t[i][:, first : first + count], tb_t[(i, first // 2)][:, first % 2 : first % 2 + count])
+
+        def regroup(i):
+            if not live(i):
+                return
+            ga_t[i] = single.tile([P, 3, P, 4], BF16, name="ga", align_bytes=64)
+            nc.gpsimd.tensor_scalar(
+                out=ga_t[i][:],
+                in0=pl_t[i][:].rearrange("p g t q -> p g q t"),
+                scalar1=1.0,
+                scalar2=0.0,
+                op0=ALU.mult,
+                op1=ALU.add,
+            )
+
+        def grouped(i, eng):
+            if not live(i):
+                return
+            gb_t[i] = work.tile([P, P, 4], BF16, name="gb", align_bytes=64)
+            copy_out(eng, gb_t[i][:], tb_t[(i, 1)][:, 1].rearrange("p t q -> p q t"))
 
         def quant(i):
             if not live(i):
@@ -176,9 +199,19 @@ def tile_dotattention_kernel(tc, query, key, value, out):
             ec_t[i] = work.tile([P, NG * P], U32, name="ec", align_bytes=64)
             es_t[i] = work.tile([P, NG * P], U8, name="es", align_bytes=64)
             nc.vector.quantize_mx(
-                out=ec_t[i][:].bitcast(FP8X4),
-                scales=es_t[i][:],
-                in_=grp_t[i][:].rearrange("p g q t -> p (g q t)"),
+                out=ec_t[i][:, 3 * P :].bitcast(FP8X4),
+                scales=es_t[i][:, 3 * P :],
+                in_=gb_t[i][:].rearrange("p q t -> p (q t)"),
+            )
+            nc.vector.quantize_mx(
+                out=ec_t[i][:, : 2 * P].bitcast(FP8X4),
+                scales=es_t[i][:, : 2 * P],
+                in_=ga_t[i][:, 0:2].rearrange("p g q t -> p (g q t)"),
+            )
+            nc.vector.quantize_mx(
+                out=ec_t[i][:, 2 * P : 3 * P].bitcast(FP8X4),
+                scales=es_t[i][:, 2 * P : 3 * P],
+                in_=ga_t[i][:, 2].rearrange("p q t -> p (q t)"),
             )
 
         def pv(i):
@@ -218,27 +251,30 @@ def tile_dotattention_kernel(tc, query, key, value, out):
         prep(0, 0, "dve")
         prep(0, 1, "act")
         prep(0, 2, "dve")
+        score(0, 0)
+        score(0, 1)
         for p in range(-3, NT + 3):
-            score(p + 3, 0)
-            score(p + 3, 1)
-            flip(p, 0)
-            flip(p, 1)
+            for j in range(NG):
+                flip(p, j)
             score(p + 3, 2)
             score(p + 3, 3)
-            flip(p, 2)
-            flip(p, 3)
             pv(p - 2)
             leave(p + 3, 0)
+            if p % 2 == 0:
+                planes(p, 2, 1, "dve")
             leave(p + 3, 1)
-            quant(p - 1)
+            score(p + 4, 0)
+            score(p + 4, 1)
             expo(p + 1, 0)
-            evac(p, 0, "act")
-            evac(p, 1, "act")
+            planes(p, 0, 2, "act")
+            if p % 2 == 1:
+                planes(p, 2, 1, "act")
+            quant(p - 1)
+            regroup(p)
+            grouped(p, "act")
             leave(p + 3, 2)
             leave(p + 3, 3)
             expo(p + 1, 1)
-            evac(p, 2, "act")
-            evac(p, 3, "dve")
             finish(p - 2)
             if p == -3:
                 prep(0, 3, "act")

@@ -21,8 +21,6 @@ NG = 4
 NT = H * NQ
 FLOPS = 2 * 2 * H * S * S * D
 
-PREP_AT = {2: 0, 4: 1, 6: 2, 8: 3, 10: 4}
-
 
 def tile_dotattention_kernel(tc, query, key, value, out):
     nc = tc.nc
@@ -32,7 +30,6 @@ def tile_dotattention_kernel(tc, query, key, value, out):
         keep = ctx.enter_context(tc.tile_pool(name="keep", bufs=2))
         work = ctx.enter_context(tc.tile_pool(name="work", bufs=3))
         deep = ctx.enter_context(tc.tile_pool(name="deep", bufs=4))
-        pair = ctx.enter_context(tc.tile_pool(name="pair", bufs=2))
         single = ctx.enter_context(tc.tile_pool(name="single", bufs=1))
         small = ctx.enter_context(tc.tile_pool(name="small", bufs=4))
         ps_s = ctx.enter_context(tc.psum_pool(name="ps_s", bufs=4))
@@ -58,44 +55,50 @@ def tile_dotattention_kernel(tc, query, key, value, out):
         nc.vector.memset(warm[:], 0.0)
         nc.scalar.activation(out=warm[:], in_=warm[:], func=ACT.Exp)
 
-        kT, qT, v_codes, v_scales = {}, {}, {}, {}
+        kT, qT, vg_t, v_codes, v_scales = {}, {}, {}, {}, {}
 
-        def prep(h, piece, eng):
+        def copy_out(eng, dst, src):
+            if eng == "act":
+                nc.scalar.copy(out=dst, in_=src)
+            else:
+                nc.vector.tensor_copy(out=dst, in_=src)
+
+        def prep_qk(h, piece, eng):
             if piece == 0:
                 kT[h] = keep.tile([P, S], BF16, name="kt")
                 qT[h] = keep.tile([P, S], BF16, name="qt")
-            if piece < 4:
-                half = piece % 2
-                tb = ps_t.tile([P, 2, 4, P], BF16, name="tb")
-                for a in range(8):
-                    if piece < 2:
-                        src = k_raw[h][:, 2 * half + a // 4, a % 4, :]
-                    else:
-                        c = 8 * half + a
-                        src = q_raw[h][:, c * D : (c + 1) * D]
-                    nc.tensor.transpose(tb[:, a // 4, a % 4, :], src, ident[:])
-                dst = (kT[h] if piece < 2 else qT[h])[:, half * 1024 : (half + 1) * 1024]
-                if eng == "act":
-                    nc.scalar.copy(out=dst, in_=tb[:].rearrange("p a b c -> p (a b c)"))
+            half = piece % 2
+            tb = ps_t.tile([P, 2, 4, P], BF16, name="tb")
+            for a in range(8):
+                if piece < 2:
+                    src = k_raw[h][:, 2 * half + a // 4, a % 4, :]
                 else:
-                    nc.vector.tensor_copy(out=dst, in_=tb[:].rearrange("p a b c -> p (a b c)"))
-            else:
-                vg = work.tile([P, NG, D, 4], BF16, name="vg", align_bytes=64)
-                nc.gpsimd.tensor_scalar(
-                    out=vg[:],
-                    in0=v_raw[h][:].rearrange("p g t d -> p g d t"),
-                    scalar1=1.0,
-                    scalar2=0.0,
-                    op0=ALU.mult,
-                    op1=ALU.add,
-                )
-                v_codes[h] = keep.tile([P, NG * D], U32, name="vc", align_bytes=64)
-                v_scales[h] = keep.tile([P, NG * D], U8, name="vs", align_bytes=64)
-                nc.vector.quantize_mx(
-                    out=v_codes[h][:].bitcast(FP8X4),
-                    scales=v_scales[h][:],
-                    in_=vg[:].rearrange("p g d t -> p (g d t)"),
-                )
+                    c = 8 * half + a
+                    src = q_raw[h][:, c * D : (c + 1) * D]
+                nc.tensor.transpose(tb[:, a // 4, a % 4, :], src, ident[:])
+            dst = (kT[h] if piece < 2 else qT[h])[:, half * 1024 : (half + 1) * 1024]
+            copy_out(eng, dst, tb[:].rearrange("p a b c -> p (a b c)"))
+
+        def prep_v(h, g):
+            if g == 0:
+                vg_t[h] = keep.tile([P, NG, D, 4], BF16, name="vg", align_bytes=64)
+            nc.gpsimd.tensor_scalar(
+                out=vg_t[h][:, g],
+                in0=v_raw[h][:, g].rearrange("p t d -> p d t"),
+                scalar1=1.0,
+                scalar2=0.0,
+                op0=ALU.mult,
+                op1=ALU.add,
+            )
+
+        def quant_v(h):
+            v_codes[h] = keep.tile([P, NG * D], U32, name="vc", align_bytes=64)
+            v_scales[h] = keep.tile([P, NG * D], U8, name="vs", align_bytes=64)
+            nc.vector.quantize_mx(
+                out=v_codes[h][:].bitcast(FP8X4),
+                scales=v_scales[h][:],
+                in_=vg_t[h][:].rearrange("p g d t -> p (g d t)"),
+            )
 
         s_t, sb_t, mn_t, nm_t, rs_t, e_t, tb_t, pl_t, ga_t, gb_t, ec_t, es_t, o_t = {}, {}, {}, {}, {}, {}, {}, {}, {}, {}, {}, {}, {}
 
@@ -134,50 +137,40 @@ def tile_dotattention_kernel(tc, query, key, value, out):
                 nm_t[i] = small.tile([P, 1], F32, name="nm")
                 nc.vector.tensor_reduce(out=nm_t[i][:], in_=mn_t[i][:], axis=AX.X, op=ALU.min)
 
-        def expo(i, half):
+        def expo(i):
             if not live(i):
                 return
-            if half == 0:
-                if i % 4 == 0:
-                    rs_t[i // 4] = small.tile([P, 4, 2], F32, name="rs")
-                e_t[i] = work.tile([P, S], BF16, name="e")
-            cols = slice(half * 1024, (half + 1) * 1024)
+            if i % 4 == 0:
+                rs_t[i // 4] = small.tile([P, 4], F32, name="rs")
+            e_t[i] = work.tile([P, S], BF16, name="e")
             nc.scalar.activation(
-                out=e_t[i][:, cols],
-                in_=sb_t[i][:, cols],
+                out=e_t[i][:],
+                in_=sb_t[i][:],
                 func=ACT.Exp,
                 bias=nm_t[i][:, 0:1],
                 scale=-1.0,
-                accum_out=rs_t[i // 4][:, i % 4, half : half + 1],
+                accum_out=rs_t[i // 4][:, i % 4 : i % 4 + 1],
             )
 
-        def flip(i, j):
+        def flip(i, half):
             if not live(i):
                 return
-            if j % 2 == 0:
-                tb_t[(i, j // 2)] = ps_t.tile([P, 2, 4, P], BF16, name="tb")
-            tb = tb_t[(i, j // 2)]
-            for t in range(4):
-                c = 4 * j + t
-                nc.tensor.transpose(tb[:, j % 2, t, :], e_t[i][:, c * P : (c + 1) * P], ident[:])
+            tb = ps_t.tile([P, 2, 4, P], BF16, name="tb")
+            tb_t[(i, half)] = tb
+            for a in range(8):
+                c = 8 * half + a
+                nc.tensor.transpose(tb[:, a // 4, a % 4, :], e_t[i][:, c * P : (c + 1) * P], ident[:])
 
-        def copy_out(eng, dst, src):
-            if eng == "act":
-                nc.scalar.copy(out=dst, in_=src)
-            else:
-                nc.vector.tensor_copy(out=dst, in_=src)
-
-        def planes(i, first, count, eng):
+        def planes(i):
             if not live(i):
                 return
-            if i not in pl_t:
-                pl_t[i] = pair.tile([P, 3, 4, P], BF16, name="pl")
-            copy_out(eng, pl_t[i][:, first : first + count], tb_t[(i, first // 2)][:, first % 2 : first % 2 + count])
+            pl_t[i] = work.tile([P, 2, 4, P], BF16, name="pl")
+            copy_out("act", pl_t[i][:], tb_t[(i, 0)][:])
 
         def regroup(i):
             if not live(i):
                 return
-            ga_t[i] = single.tile([P, 3, P, 4], BF16, name="ga", align_bytes=64)
+            ga_t[i] = single.tile([P, 2, P, 4], BF16, name="ga", align_bytes=64)
             nc.gpsimd.tensor_scalar(
                 out=ga_t[i][:],
                 in0=pl_t[i][:].rearrange("p g t q -> p g q t"),
@@ -190,8 +183,8 @@ def tile_dotattention_kernel(tc, query, key, value, out):
         def grouped(i, eng):
             if not live(i):
                 return
-            gb_t[i] = work.tile([P, P, 4], BF16, name="gb", align_bytes=64)
-            copy_out(eng, gb_t[i][:], tb_t[(i, 1)][:, 1].rearrange("p t q -> p q t"))
+            gb_t[i] = work.tile([P, 2, P, 4], BF16, name="gb", align_bytes=64)
+            copy_out(eng, gb_t[i][:], tb_t[(i, 1)][:].rearrange("p g t q -> p g q t"))
 
         def quant(i):
             if not live(i):
@@ -199,19 +192,14 @@ def tile_dotattention_kernel(tc, query, key, value, out):
             ec_t[i] = work.tile([P, NG * P], U32, name="ec", align_bytes=64)
             es_t[i] = work.tile([P, NG * P], U8, name="es", align_bytes=64)
             nc.vector.quantize_mx(
-                out=ec_t[i][:, 3 * P :].bitcast(FP8X4),
-                scales=es_t[i][:, 3 * P :],
-                in_=gb_t[i][:].rearrange("p q t -> p (q t)"),
+                out=ec_t[i][:, 2 * P :].bitcast(FP8X4),
+                scales=es_t[i][:, 2 * P :],
+                in_=gb_t[i][:].rearrange("p g q t -> p (g q t)"),
             )
             nc.vector.quantize_mx(
                 out=ec_t[i][:, : 2 * P].bitcast(FP8X4),
                 scales=es_t[i][:, : 2 * P],
-                in_=ga_t[i][:, 0:2].rearrange("p g q t -> p (g q t)"),
-            )
-            nc.vector.quantize_mx(
-                out=ec_t[i][:, 2 * P : 3 * P].bitcast(FP8X4),
-                scales=es_t[i][:, 2 * P : 3 * P],
-                in_=ga_t[i][:, 2].rearrange("p q t -> p (q t)"),
+                in_=ga_t[i][:].rearrange("p g q t -> p (g q t)"),
             )
 
         def pv(i):
@@ -236,10 +224,8 @@ def tile_dotattention_kernel(tc, query, key, value, out):
             if not live(i) or i % 4 != 3:
                 return
             h, n = divmod(i, NQ)
-            tot = small.tile([P, 4], F32, name="tot")
-            nc.vector.tensor_reduce(out=tot[:], in_=rs_t[i // 4][:], axis=AX.X, op=ALU.add)
             rc = small.tile([P, 4], F32, name="rc")
-            nc.vector.reciprocal(out=rc[:], in_=tot[:])
+            nc.vector.reciprocal(out=rc[:], in_=rs_t[i // 4][:])
             ob = small.tile([P, 4, D], F32, name="ob")
             nc.vector.tensor_tensor(
                 out=ob[:], in0=o_t[i // 4][:], in1=rc[:].unsqueeze(2).to_broadcast([P, 4, D]), op=ALU.mult
@@ -248,39 +234,40 @@ def tile_dotattention_kernel(tc, query, key, value, out):
                 out=out[0, h].rearrange("(p n) d -> p n d", n=NQ)[:, n - 3 : n + 1, :], in_=ob[:]
             )
 
-        prep(0, 0, "dve")
-        prep(0, 1, "act")
-        prep(0, 2, "dve")
+        prep_qk(0, 0, "dve")
+        prep_qk(0, 1, "act")
+        prep_qk(0, 2, "dve")
         score(0, 0)
         score(0, 1)
         for p in range(-3, NT + 3):
-            for j in range(NG):
-                flip(p, j)
             score(p + 3, 2)
             score(p + 3, 3)
             pv(p - 2)
             leave(p + 3, 0)
-            if p % 2 == 0:
-                planes(p, 2, 1, "dve")
-            leave(p + 3, 1)
             score(p + 4, 0)
+            leave(p + 3, 1)
             score(p + 4, 1)
-            expo(p + 1, 0)
-            planes(p, 0, 2, "act")
-            if p % 2 == 1:
-                planes(p, 2, 1, "act")
+            expo(p + 1)
+            planes(p)
+            flip(p + 1, 0)
             quant(p - 1)
             regroup(p)
-            grouped(p, "act")
             leave(p + 3, 2)
             leave(p + 3, 3)
-            expo(p + 1, 1)
+            grouped(p, "dve" if p % 4 == 3 else "act")
+            flip(p + 1, 1)
             finish(p - 2)
             if p == -3:
-                prep(0, 3, "act")
+                prep_qk(0, 3, "act")
+                for g in range(NG):
+                    prep_v(0, g)
             if p == -2:
-                prep(0, 4, "dve")
-            if live(p):
-                h, n = divmod(p, NQ)
-                if n in PREP_AT and h + 1 < H:
-                    prep(h + 1, PREP_AT[n], "dve" if PREP_AT[n] % 2 else "act")
+                quant_v(0)
+            h, n = divmod(p, NQ)
+            if 0 <= h < H - 1:
+                if n % 2 == 1 and n < 8:
+                    prep_qk(h + 1, n // 2, "dve" if n % 4 == 1 else "act")
+                if 8 <= n < 12:
+                    prep_v(h + 1, n - 8)
+                if n == 12:
+                    quant_v(h + 1)

@@ -165,7 +165,7 @@ def tile_dotattention_kernel(tc, query, key, value, out):
             if not live(i):
                 return
             pl_t[i] = work.tile([P, 2, 4, P], BF16, name="pl")
-            copy_out("act", pl_t[i][:], tb_t[(i, 0)][:])
+            copy_out("dve", pl_t[i][:], tb_t[(i, 0)][:])
 
         def regroup(i):
             if not live(i):
@@ -243,18 +243,18 @@ def tile_dotattention_kernel(tc, query, key, value, out):
             score(p + 3, 2)
             score(p + 3, 3)
             pv(p - 2)
+            planes(p)
             leave(p + 3, 0)
             score(p + 4, 0)
             leave(p + 3, 1)
             score(p + 4, 1)
             expo(p + 1)
-            planes(p)
             flip(p + 1, 0)
             quant(p - 1)
             regroup(p)
             leave(p + 3, 2)
             leave(p + 3, 3)
-            grouped(p, "dve" if p % 4 == 3 else "act")
+            grouped(p, "act")
             flip(p + 1, 1)
             finish(p - 2)
             if p == -3:

@@ -30,7 +30,6 @@ def tile_dotattention_kernel(tc, query, key, value, out):
         keep = ctx.enter_context(tc.tile_pool(name="keep", bufs=2))
         work = ctx.enter_context(tc.tile_pool(name="work", bufs=3))
         deep = ctx.enter_context(tc.tile_pool(name="deep", bufs=4))
-        single = ctx.enter_context(tc.tile_pool(name="single", bufs=1))
         small = ctx.enter_context(tc.tile_pool(name="small", bufs=4))
         ps_s = ctx.enter_context(tc.psum_pool(name="ps_s", bufs=4))
         ps_t = ctx.enter_context(tc.psum_pool(name="ps_t", bufs=3))
@@ -40,9 +39,11 @@ def tile_dotattention_kernel(tc, query, key, value, out):
         q_raw, k_raw, v_raw = [], [], []
         for h in range(H):
             kr = raw.tile([P, NG, 4, D], BF16, name="kr")
-            nc.sync.dma_start(out=kr[:], in_=key[0, h].rearrange("(g p t) d -> p g t d", g=NG, t=4))
+            k_view = key[0, h].rearrange("(g p t) d -> p g t d", g=NG, t=4)
+            nc.sync.dma_start(out=kr[:, 0:2], in_=k_view[:, 0:2])
             qr = raw.tile([P, NQ * D], BF16, name="qr")
             nc.sync.dma_start(out=qr[:], in_=query[0, h].rearrange("(p n) d -> p (n d)", n=NQ))
+            nc.sync.dma_start(out=kr[:, 2:4], in_=k_view[:, 2:4])
             vr = raw.tile([P, NG, 4, D], BF16, name="vr")
             nc.sync.dma_start(out=vr[:], in_=value[0, h].rearrange("(g p t) d -> p g t d", g=NG, t=4))
             k_raw.append(kr)
@@ -100,7 +101,7 @@ def tile_dotattention_kernel(tc, query, key, value, out):
                 in_=vg_t[h][:].rearrange("p g d t -> p (g d t)"),
             )
 
-        s_t, sb_t, mn_t, nm_t, rs_t, e_t, tb_t, pl_t, ga_t, gb_t, ec_t, es_t, o_t = {}, {}, {}, {}, {}, {}, {}, {}, {}, {}, {}, {}, {}
+        s_t, sb_t, mn_t, nm_t, rs_t, e_t, tb_t, pl_t, grp_t, ec_t, es_t, o_t = {}, {}, {}, {}, {}, {}, {}, {}, {}, {}, {}, {}
 
         def live(i):
             return 0 <= i < NT
@@ -157,22 +158,26 @@ def tile_dotattention_kernel(tc, query, key, value, out):
                 return
             tb = ps_t.tile([P, 2, 4, P], BF16, name="tb")
             tb_t[(i, half)] = tb
+            if half == 0:
+                grp_t[i] = work.tile([P, NG, P, 4], BF16, name="grp", align_bytes=64)
             for a in range(8):
                 c = 8 * half + a
                 nc.tensor.transpose(tb[:, a // 4, a % 4, :], e_t[i][:, c * P : (c + 1) * P], ident[:])
 
+        def both_on_scalar(i):
+            return i % 2 == 1
+
         def planes(i):
-            if not live(i):
+            if not live(i) or both_on_scalar(i):
                 return
             pl_t[i] = work.tile([P, 2, 4, P], BF16, name="pl")
-            copy_out("dve", pl_t[i][:], tb_t[(i, 0)][:])
+            nc.vector.tensor_copy(out=pl_t[i][:], in_=tb_t[(i, 0)][:])
 
         def regroup(i):
-            if not live(i):
+            if not live(i) or both_on_scalar(i):
                 return
-            ga_t[i] = single.tile([P, 2, P, 4], BF16, name="ga", align_bytes=64)
             nc.gpsimd.tensor_scalar(
-                out=ga_t[i][:],
+                out=grp_t[i][:, 0:2],
                 in0=pl_t[i][:].rearrange("p g t q -> p g q t"),
                 scalar1=1.0,
                 scalar2=0.0,
@@ -180,11 +185,12 @@ def tile_dotattention_kernel(tc, query, key, value, out):
                 op1=ALU.add,
             )
 
-        def grouped(i, eng):
-            if not live(i):
+        def grouped(i, half):
+            if not live(i) or (half == 0 and not both_on_scalar(i)):
                 return
-            gb_t[i] = work.tile([P, 2, P, 4], BF16, name="gb", align_bytes=64)
-            copy_out(eng, gb_t[i][:], tb_t[(i, 1)][:].rearrange("p g t q -> p g q t"))
+            nc.scalar.copy(
+                out=grp_t[i][:, 2 * half : 2 * half + 2], in_=tb_t[(i, half)][:].rearrange("p g t q -> p g q t")
+            )
 
         def quant(i):
             if not live(i):
@@ -192,14 +198,9 @@ def tile_dotattention_kernel(tc, query, key, value, out):
             ec_t[i] = work.tile([P, NG * P], U32, name="ec", align_bytes=64)
             es_t[i] = work.tile([P, NG * P], U8, name="es", align_bytes=64)
             nc.vector.quantize_mx(
-                out=ec_t[i][:, 2 * P :].bitcast(FP8X4),
-                scales=es_t[i][:, 2 * P :],
-                in_=gb_t[i][:].rearrange("p g q t -> p (g q t)"),
-            )
-            nc.vector.quantize_mx(
-                out=ec_t[i][:, : 2 * P].bitcast(FP8X4),
-                scales=es_t[i][:, : 2 * P],
-                in_=ga_t[i][:].rearrange("p g q t -> p (g q t)"),
+                out=ec_t[i][:].bitcast(FP8X4),
+                scales=es_t[i][:],
+                in_=grp_t[i][:].rearrange("p g q t -> p (g q t)"),
             )
 
         def pv(i):
@@ -235,39 +236,41 @@ def tile_dotattention_kernel(tc, query, key, value, out):
             )
 
         prep_qk(0, 0, "dve")
-        prep_qk(0, 1, "act")
-        prep_qk(0, 2, "dve")
+        prep_qk(0, 2, "act")
         score(0, 0)
         score(0, 1)
+        prep_qk(0, 1, "dve")
         for p in range(-3, NT + 3):
+            h, n = divmod(p, NQ)
+            ahead = 0 <= h < H - 1
             score(p + 3, 2)
             score(p + 3, 3)
             pv(p - 2)
-            planes(p)
             leave(p + 3, 0)
             score(p + 4, 0)
             leave(p + 3, 1)
             score(p + 4, 1)
             expo(p + 1)
-            flip(p + 1, 0)
+            grouped(p, 0)
             quant(p - 1)
+            if p == -2:
+                quant_v(0)
+            if ahead and n == 12:
+                quant_v(h + 1)
+            planes(p)
             regroup(p)
+            if p == -3:
+                for g in range(NG):
+                    prep_v(0, g)
+            if ahead and 8 <= n < 12:
+                prep_v(h + 1, n - 8)
+            flip(p + 1, 0)
             leave(p + 3, 2)
             leave(p + 3, 3)
-            grouped(p, "act")
+            grouped(p, 1)
             flip(p + 1, 1)
             finish(p - 2)
             if p == -3:
                 prep_qk(0, 3, "act")
-                for g in range(NG):
-                    prep_v(0, g)
-            if p == -2:
-                quant_v(0)
-            h, n = divmod(p, NQ)
-            if 0 <= h < H - 1:
-                if n % 2 == 1 and n < 8:
-                    prep_qk(h + 1, n // 2, "dve" if n % 4 == 1 else "act")
-                if 8 <= n < 12:
-                    prep_v(h + 1, n - 8)
-                if n == 12:
-                    quant_v(h + 1)
+            if ahead and n % 2 == 1 and n < 8:
+                prep_qk(h + 1, n // 2, "dve" if n % 4 == 1 else "act")

@@ -13,12 +13,16 @@ ALU = mybir.AluOpType
 ACT = mybir.ActivationFunctionType
 
 P = 128
+PACK = 4
 H = 4
 S = 2048
 D = 128
-NQ = S // P
-NG = 4
-NT = H * NQ
+TILES = S // P
+PASSES = S // (P * PACK)
+BANK = 512
+HALF = S // 2
+GROUP = 4
+NT = H * TILES
 FLOPS = 2 * 2 * H * S * S * D
 
 
@@ -31,21 +35,21 @@ def tile_dotattention_kernel(tc, query, key, value, out):
         work = ctx.enter_context(tc.tile_pool(name="work", bufs=3))
         deep = ctx.enter_context(tc.tile_pool(name="deep", bufs=4))
         small = ctx.enter_context(tc.tile_pool(name="small", bufs=4))
-        ps_s = ctx.enter_context(tc.psum_pool(name="ps_s", bufs=4))
+        ps_s = ctx.enter_context(tc.psum_pool(name="ps_s", bufs=PASSES))
         ps_t = ctx.enter_context(tc.psum_pool(name="ps_t", bufs=3))
         ps_o = ctx.enter_context(tc.psum_pool(name="ps_o", bufs=1))
         ctx.enter_context(tc.manual_schedule())
 
         q_raw, k_raw, v_raw = [], [], []
         for h in range(H):
-            kr = raw.tile([P, NG, 4, D], BF16, name="kr")
-            k_view = key[0, h].rearrange("(g p t) d -> p g t d", g=NG, t=4)
+            kr = raw.tile([P, PASSES, PACK, D], BF16, name="kr")
+            k_view = key[0, h].rearrange("(g p t) d -> p g t d", g=PASSES, t=PACK)
             nc.sync.dma_start(out=kr[:, 0:2], in_=k_view[:, 0:2])
-            qr = raw.tile([P, NQ * D], BF16, name="qr")
-            nc.sync.dma_start(out=qr[:], in_=query[0, h].rearrange("(p n) d -> p (n d)", n=NQ))
+            qr = raw.tile([P, TILES * D], BF16, name="qr")
+            nc.sync.dma_start(out=qr[:], in_=query[0, h].rearrange("(p n) d -> p (n d)", n=TILES))
             nc.sync.dma_start(out=kr[:, 2:4], in_=k_view[:, 2:4])
-            vr = raw.tile([P, NG, 4, D], BF16, name="vr")
-            nc.sync.dma_start(out=vr[:], in_=value[0, h].rearrange("(g p t) d -> p g t d", g=NG, t=4))
+            vr = raw.tile([P, PASSES, PACK, D], BF16, name="vr")
+            nc.sync.dma_start(out=vr[:], in_=value[0, h].rearrange("(g p t) d -> p g t d", g=PASSES, t=PACK))
             k_raw.append(kr)
             q_raw.append(qr)
             v_raw.append(vr)
@@ -56,35 +60,31 @@ def tile_dotattention_kernel(tc, query, key, value, out):
         nc.vector.memset(warm[:], 0.0)
         nc.scalar.activation(out=warm[:], in_=warm[:], func=ACT.Exp)
 
-        kT, qT, vg_t, v_codes, v_scales = {}, {}, {}, {}, {}
+        kT, qT, v_grouped, v_codes, v_scales = {}, {}, {}, {}, {}
 
-        def copy_out(eng, dst, src):
-            if eng == "act":
-                nc.scalar.copy(out=dst, in_=src)
-            else:
-                nc.vector.tensor_copy(out=dst, in_=src)
-
-        def prep_qk(h, piece, eng):
-            if piece == 0:
+        def transpose_half(h, name, half):
+            if h not in kT:
                 kT[h] = keep.tile([P, S], BF16, name="kt")
                 qT[h] = keep.tile([P, S], BF16, name="qt")
-            half = piece % 2
-            tb = ps_t.tile([P, 2, 4, P], BF16, name="tb")
-            for a in range(8):
-                if piece < 2:
-                    src = k_raw[h][:, 2 * half + a // 4, a % 4, :]
+            bank = ps_t.tile([P, 2, PACK, P], BF16, name="tb")
+            for a in range(2 * PACK):
+                if name == "key":
+                    rows = k_raw[h][:, 2 * half + a // PACK, a % PACK, :]
                 else:
-                    c = 8 * half + a
-                    src = q_raw[h][:, c * D : (c + 1) * D]
-                nc.tensor.transpose(tb[:, a // 4, a % 4, :], src, ident[:])
-            dst = (kT[h] if piece < 2 else qT[h])[:, half * 1024 : (half + 1) * 1024]
-            copy_out(eng, dst, tb[:].rearrange("p a b c -> p (a b c)"))
+                    n = 2 * PACK * half + a
+                    rows = q_raw[h][:, n * D : (n + 1) * D]
+                nc.tensor.transpose(bank[:, a // PACK, a % PACK, :], rows, ident[:])
+            cols = slice(half * HALF, (half + 1) * HALF)
+            if name == "key":
+                nc.vector.tensor_copy(out=kT[h][:, cols], in_=bank[:].rearrange("p a b c -> p (a b c)"))
+            else:
+                nc.scalar.copy(out=qT[h][:, cols], in_=bank[:].rearrange("p a b c -> p (a b c)"))
 
-        def prep_v(h, g):
+        def group_value(h, g):
             if g == 0:
-                vg_t[h] = keep.tile([P, NG, D, 4], BF16, name="vg", align_bytes=64)
+                v_grouped[h] = keep.tile([P, PASSES, D, PACK], BF16, name="vg", align_bytes=64)
             nc.gpsimd.tensor_scalar(
-                out=vg_t[h][:, g],
+                out=v_grouped[h][:, g],
                 in0=v_raw[h][:, g].rearrange("p t d -> p d t"),
                 scalar1=1.0,
                 scalar2=0.0,
@@ -92,185 +92,188 @@ def tile_dotattention_kernel(tc, query, key, value, out):
                 op1=ALU.add,
             )
 
-        def quant_v(h):
-            v_codes[h] = keep.tile([P, NG * D], U32, name="vc", align_bytes=64)
-            v_scales[h] = keep.tile([P, NG * D], U8, name="vs", align_bytes=64)
+        def quantise_value(h):
+            v_codes[h] = keep.tile([P, PASSES * D], U32, name="vc", align_bytes=64)
+            v_scales[h] = keep.tile([P, PASSES * D], U8, name="vs", align_bytes=64)
             nc.vector.quantize_mx(
                 out=v_codes[h][:].bitcast(FP8X4),
                 scales=v_scales[h][:],
-                in_=vg_t[h][:].rearrange("p g d t -> p (g d t)"),
+                in_=v_grouped[h][:].rearrange("p g d t -> p (g d t)"),
             )
 
-        s_t, sb_t, mn_t, nm_t, rs_t, e_t, tb_t, pl_t, grp_t, ec_t, es_t, o_t = {}, {}, {}, {}, {}, {}, {}, {}, {}, {}, {}, {}
+        score_bank, neg_score, bank_min, neg_max, row_sum, e_bf16 = {}, {}, {}, {}, {}, {}
+        plane_bank, planes, grouped, e_codes, e_scales, out_bank = {}, {}, {}, {}, {}, {}
 
         def live(i):
             return 0 <= i < NT
 
+        def route(i):
+            if i >= NT - 3:
+                return ("vector", "scalar" if i == NT - 1 else "vector")
+            if i % 3 == 2:
+                return ("scalar", "scalar")
+            return ("gpsimd", "scalar")
+
         def score(i, j):
             if not live(i):
                 return
-            h, n = divmod(i, NQ)
-            s_t[(i, j)] = ps_s.tile([P, 512], F32, name="s")
+            h, n = divmod(i, TILES)
+            score_bank[(i, j)] = ps_s.tile([P, BANK], F32, name="s")
             nc.tensor.matmul(
-                out=s_t[(i, j)][:],
+                out=score_bank[(i, j)][:],
                 lhsT=qT[h][:, n * P : (n + 1) * P],
-                rhs=kT[h][:, j * 512 : (j + 1) * 512],
+                rhs=kT[h][:, j * BANK : (j + 1) * BANK],
                 start=True,
                 stop=True,
             )
 
-        def leave(i, j):
+        def score_out(i, j):
             if not live(i):
                 return
             if j == 0:
-                mn_t[i] = small.tile([P, NG], F32, name="mn")
-                sb_t[i] = deep.tile([P, S], F32, name="sb")
+                bank_min[i] = small.tile([P, PASSES], F32, name="mn")
+                neg_score[i] = deep.tile([P, S], F32, name="sb")
             nc.vector.tensor_scalar(
-                out=sb_t[i][:, j * 512 : (j + 1) * 512],
-                in0=s_t[(i, j)][:],
+                out=neg_score[i][:, j * BANK : (j + 1) * BANK],
+                in0=score_bank[(i, j)][:],
                 scalar1=-1.0 / D,
                 scalar2=None,
                 op0=ALU.mult,
                 op1=ALU.min,
-                accum_out=mn_t[i][:, j : j + 1],
+                accum_out=bank_min[i][:, j : j + 1],
             )
-            if j == NG - 1:
-                nm_t[i] = small.tile([P, 1], F32, name="nm")
-                nc.vector.tensor_reduce(out=nm_t[i][:], in_=mn_t[i][:], axis=AX.X, op=ALU.min)
+            if j == PASSES - 1:
+                neg_max[i] = small.tile([P, 1], F32, name="nm")
+                nc.vector.tensor_reduce(out=neg_max[i][:], in_=bank_min[i][:], axis=AX.X, op=ALU.min)
 
-        def expo(i):
+        def exponential(i):
             if not live(i):
                 return
-            if i % 4 == 0:
-                rs_t[i // 4] = small.tile([P, 4], F32, name="rs")
-            e_t[i] = work.tile([P, S], BF16, name="e")
+            if i % GROUP == 0:
+                row_sum[i // GROUP] = small.tile([P, GROUP], F32, name="rs")
+            e_bf16[i] = work.tile([P, S], BF16, name="e")
             nc.scalar.activation(
-                out=e_t[i][:],
-                in_=sb_t[i][:],
+                out=e_bf16[i][:],
+                in_=neg_score[i][:],
                 func=ACT.Exp,
-                bias=nm_t[i][:, 0:1],
+                bias=neg_max[i][:, 0:1],
                 scale=-1.0,
-                accum_out=rs_t[i // 4][:, i % 4 : i % 4 + 1],
+                accum_out=row_sum[i // GROUP][:, i % GROUP : i % GROUP + 1],
             )
 
-        def flip(i, half):
+        def transpose_e(i, half):
             if not live(i):
                 return
-            tb = ps_t.tile([P, 2, 4, P], BF16, name="tb")
-            tb_t[(i, half)] = tb
+            bank = ps_t.tile([P, 2, PACK, P], BF16, name="tb")
+            plane_bank[(i, half)] = bank
             if half == 0:
-                grp_t[i] = work.tile([P, NG, P, 4], BF16, name="grp", align_bytes=64)
-            for a in range(8):
-                c = 8 * half + a
-                nc.tensor.transpose(tb[:, a // 4, a % 4, :], e_t[i][:, c * P : (c + 1) * P], ident[:])
+                grouped[i] = work.tile([P, PASSES, P, PACK], BF16, name="grp", align_bytes=64)
+            for a in range(2 * PACK):
+                c = 2 * PACK * half + a
+                nc.tensor.transpose(bank[:, a // PACK, a % PACK, :], e_bf16[i][:, c * P : (c + 1) * P], ident[:])
 
-        def both_on_scalar(i):
-            return i % 2 == 1
-
-        def planes(i):
-            if not live(i) or both_on_scalar(i):
-                return
-            pl_t[i] = work.tile([P, 2, 4, P], BF16, name="pl")
-            nc.vector.tensor_copy(out=pl_t[i][:], in_=tb_t[(i, 0)][:])
-
-        def regroup(i):
-            if not live(i) or both_on_scalar(i):
-                return
-            nc.gpsimd.tensor_scalar(
-                out=grp_t[i][:, 0:2],
-                in0=pl_t[i][:].rearrange("p g t q -> p g q t"),
-                scalar1=1.0,
-                scalar2=0.0,
-                op0=ALU.mult,
-                op1=ALU.add,
-            )
-
-        def grouped(i, half):
-            if not live(i) or (half == 0 and not both_on_scalar(i)):
-                return
-            nc.scalar.copy(
-                out=grp_t[i][:, 2 * half : 2 * half + 2], in_=tb_t[(i, half)][:].rearrange("p g t q -> p g q t")
-            )
-
-        def quant(i):
+        def planes_out(i, half):
             if not live(i):
                 return
-            ec_t[i] = work.tile([P, NG * P], U32, name="ec", align_bytes=64)
-            es_t[i] = work.tile([P, NG * P], U8, name="es", align_bytes=64)
+            way = route(i)[half]
+            bank = plane_bank[(i, half)]
+            dst = grouped[i][:, 2 * half : 2 * half + 2]
+            if way == "scalar":
+                nc.scalar.copy(out=dst, in_=bank[:].rearrange("p g t q -> p g q t"))
+            elif way == "vector":
+                nc.vector.tensor_copy(out=dst, in_=bank[:].rearrange("p g t q -> p g q t"))
+            else:
+                planes[i] = work.tile([P, 2, PACK, P], BF16, name="pl")
+                nc.vector.tensor_copy(out=planes[i][:], in_=bank[:])
+                nc.gpsimd.tensor_scalar(
+                    out=dst,
+                    in0=planes[i][:].rearrange("p g t q -> p g q t"),
+                    scalar1=1.0,
+                    scalar2=0.0,
+                    op0=ALU.mult,
+                    op1=ALU.add,
+                )
+
+        def quantise_e(i):
+            if not live(i):
+                return
+            e_codes[i] = work.tile([P, PASSES * P], U32, name="ec", align_bytes=64)
+            e_scales[i] = work.tile([P, PASSES * P], U8, name="es", align_bytes=64)
             nc.vector.quantize_mx(
-                out=ec_t[i][:].bitcast(FP8X4),
-                scales=es_t[i][:],
-                in_=grp_t[i][:].rearrange("p g q t -> p (g q t)"),
+                out=e_codes[i][:].bitcast(FP8X4),
+                scales=e_scales[i][:],
+                in_=grouped[i][:].rearrange("p g q t -> p (g q t)"),
             )
 
-        def pv(i):
+        def e_times_value(i):
             if not live(i):
                 return
-            h = i // NQ
-            if i % 4 == 0:
-                o_t[i // 4] = ps_o.tile([P, 4, D], F32, name="o")
-            for g in range(NG):
+            h = i // TILES
+            if i % GROUP == 0:
+                out_bank[i // GROUP] = ps_o.tile([P, GROUP, D], F32, name="o")
+            for g in range(PASSES):
                 cols = slice(g * P, (g + 1) * P)
                 nc.tensor.matmul_mx(
-                    out=o_t[i // 4][:, i % 4, :],
-                    lhsT=ec_t[i][:, cols].bitcast(FP8X4),
-                    lhsT_scale=es_t[i][:, cols],
+                    out=out_bank[i // GROUP][:, i % GROUP, :],
+                    lhsT=e_codes[i][:, cols].bitcast(FP8X4),
+                    lhsT_scale=e_scales[i][:, cols],
                     rhs=v_codes[h][:, cols].bitcast(FP8X4),
                     rhs_scale=v_scales[h][:, cols],
                     start=(g == 0),
-                    stop=(g == NG - 1),
+                    stop=(g == PASSES - 1),
                 )
 
-        def finish(i):
-            if not live(i) or i % 4 != 3:
+        def normalise_and_store(i):
+            if not live(i) or i % GROUP != GROUP - 1:
                 return
-            h, n = divmod(i, NQ)
-            rc = small.tile([P, 4], F32, name="rc")
-            nc.vector.reciprocal(out=rc[:], in_=rs_t[i // 4][:])
-            ob = small.tile([P, 4, D], F32, name="ob")
+            h, n = divmod(i, TILES)
+            inverse = small.tile([P, GROUP], F32, name="rc")
+            nc.vector.reciprocal(out=inverse[:], in_=row_sum[i // GROUP][:])
+            result = small.tile([P, GROUP, D], F32, name="ob")
             nc.vector.tensor_tensor(
-                out=ob[:], in0=o_t[i // 4][:], in1=rc[:].unsqueeze(2).to_broadcast([P, 4, D]), op=ALU.mult
+                out=result[:],
+                in0=out_bank[i // GROUP][:],
+                in1=inverse[:].unsqueeze(2).to_broadcast([P, GROUP, D]),
+                op=ALU.mult,
             )
             nc.sync.dma_start(
-                out=out[0, h].rearrange("(p n) d -> p n d", n=NQ)[:, n - 3 : n + 1, :], in_=ob[:]
+                out=out[0, h].rearrange("(p n) d -> p n d", n=TILES)[:, n - GROUP + 1 : n + 1, :], in_=result[:]
             )
 
-        prep_qk(0, 0, "dve")
-        prep_qk(0, 2, "act")
+        transpose_half(0, "key", 0)
+        transpose_half(0, "query", 0)
         score(0, 0)
         score(0, 1)
-        prep_qk(0, 1, "dve")
+        transpose_half(0, "key", 1)
         for p in range(-3, NT + 3):
-            h, n = divmod(p, NQ)
+            h, n = divmod(p, TILES)
             ahead = 0 <= h < H - 1
             score(p + 3, 2)
             score(p + 3, 3)
-            pv(p - 2)
-            leave(p + 3, 0)
+            e_times_value(p - 2)
+            score_out(p + 3, 0)
             score(p + 4, 0)
-            leave(p + 3, 1)
+            score_out(p + 3, 1)
             score(p + 4, 1)
-            expo(p + 1)
-            grouped(p, 0)
-            quant(p - 1)
+            exponential(p + 1)
+            quantise_e(p - 1)
             if p == -2:
-                quant_v(0)
+                quantise_value(0)
             if ahead and n == 12:
-                quant_v(h + 1)
-            planes(p)
-            regroup(p)
+                quantise_value(h + 1)
+            planes_out(p, 0)
             if p == -3:
-                for g in range(NG):
-                    prep_v(0, g)
-            if ahead and 8 <= n < 12:
-                prep_v(h + 1, n - 8)
-            flip(p + 1, 0)
-            leave(p + 3, 2)
-            leave(p + 3, 3)
-            grouped(p, 1)
-            flip(p + 1, 1)
-            finish(p - 2)
+                for g in range(PASSES):
+                    group_value(0, g)
+            if ahead and 8 <= n < 8 + PASSES:
+                group_value(h + 1, n - 8)
+            transpose_e(p + 1, 0)
+            score_out(p + 3, 2)
+            score_out(p + 3, 3)
+            planes_out(p, 1)
+            transpose_e(p + 1, 1)
+            normalise_and_store(p - 2)
             if p == -3:
-                prep_qk(0, 3, "act")
+                transpose_half(0, "query", 1)
             if ahead and n % 2 == 1 and n < 8:
-                prep_qk(h + 1, n // 2, "dve" if n % 4 == 1 else "act")
+                transpose_half(h + 1, "key" if n < 4 else "query", (n // 2) % 2)

@@ -110,7 +110,7 @@ def tile_dotattention_kernel(tc, query, key, value, out):
         def route(i):
             if i >= NT - 3:
                 return ("vector", "scalar" if i == NT - 1 else "vector")
-            if i % 3 == 2:
+            if i % 5 in (1, 3):
                 return ("scalar", "scalar")
             return ("gpsimd", "scalar")
 
@@ -143,8 +143,23 @@ def tile_dotattention_kernel(tc, query, key, value, out):
                 accum_out=bank_min[i][:, j : j + 1],
             )
             if j == PASSES - 1:
+                first_three = small.tile([P, 1], F32, name="m3")
+                nc.gpsimd.tensor_scalar(
+                    out=first_three[:],
+                    in0=bank_min[i][:, 0:1],
+                    scalar1=bank_min[i][:, 1:2],
+                    scalar2=bank_min[i][:, 2:3],
+                    op0=ALU.min,
+                    op1=ALU.min,
+                )
                 neg_max[i] = small.tile([P, 1], F32, name="nm")
-                nc.vector.tensor_reduce(out=neg_max[i][:], in_=bank_min[i][:], axis=AX.X, op=ALU.min)
+                nc.gpsimd.tensor_scalar(
+                    out=neg_max[i][:],
+                    in0=first_three[:],
+                    scalar1=bank_min[i][:, 3:4],
+                    scalar2=None,
+                    op0=ALU.min,
+                )
 
         def exponential(i):
             if not live(i):

@@ -56,6 +56,8 @@ def tile_dotattention_kernel(tc, query, key, value, out):
 
         ident = const.tile([P, P], BF16)
         make_identity(nc, ident[:])
+        ident_words = const.tile([P, P], F32)
+        make_identity(nc, ident_words[:])
         warm = const.tile([P, 1], F32)
         nc.vector.memset(warm[:], 0.0)
         nc.scalar.activation(out=warm[:], in_=warm[:], func=ACT.Exp)
@@ -76,7 +78,12 @@ def tile_dotattention_kernel(tc, query, key, value, out):
                 nc.tensor.transpose(bank[:, a // PACK, a % PACK, :], rows, ident[:])
             cols = slice(half * HALF, (half + 1) * HALF)
             if name == "key":
-                nc.vector.tensor_copy(out=kT[h][:, cols], in_=bank[:].rearrange("p a b c -> p (a b c)"))
+                for a in range(2):
+                    c0 = half * HALF + a * BANK
+                    nc.vector.tensor_copy(
+                        out=kT[h][:, c0 : c0 + BANK].rearrange("d (u p e) -> d u p e", u=2, e=2),
+                        in_=bank[:, a].rearrange("d (u e) p -> d u p e", u=2),
+                    )
             else:
                 nc.scalar.copy(out=qT[h][:, cols], in_=bank[:].rearrange("p a b c -> p (a b c)"))
 
@@ -110,9 +117,7 @@ def tile_dotattention_kernel(tc, query, key, value, out):
         def route(i):
             if i >= NT - 3:
                 return ("vector", "scalar" if i == NT - 1 else "vector")
-            if i % 5 in (1, 3):
-                return ("scalar", "scalar")
-            return ("gpsimd", "scalar")
+            return ("scalar", "scalar")
 
         def score(i, j):
             if not live(i):
@@ -179,35 +184,25 @@ def tile_dotattention_kernel(tc, query, key, value, out):
         def transpose_e(i, half):
             if not live(i):
                 return
-            bank = ps_t.tile([P, 2, PACK, P], BF16, name="tb")
+            bank = ps_t.tile([P, 2, 2, P], F32, name="tb")
             plane_bank[(i, half)] = bank
             if half == 0:
-                grouped[i] = work.tile([P, PASSES, P, PACK], BF16, name="grp", align_bytes=64)
-            for a in range(2 * PACK):
-                c = 2 * PACK * half + a
-                nc.tensor.transpose(bank[:, a // PACK, a % PACK, :], e_bf16[i][:, c * P : (c + 1) * P], ident[:])
+                grouped[i] = work.tile([P, S], BF16, name="grp", align_bytes=64)
+            words = e_bf16[i][:].bitcast(F32)
+            for a in range(4):
+                c = 4 * half + a
+                nc.tensor.transpose(bank[:, a // 2, a % 2, :], words[:, c * P : (c + 1) * P], ident_words[:])
 
         def planes_out(i, half):
             if not live(i):
                 return
             way = route(i)[half]
             bank = plane_bank[(i, half)]
-            dst = grouped[i][:, 2 * half : 2 * half + 2]
+            dst = grouped[i][:, half * HALF : (half + 1) * HALF].bitcast(F32).rearrange("p (g q u) -> p g q u", g=2, u=2)
             if way == "scalar":
-                nc.scalar.copy(out=dst, in_=bank[:].rearrange("p g t q -> p g q t"))
-            elif way == "vector":
-                nc.vector.tensor_copy(out=dst, in_=bank[:].rearrange("p g t q -> p g q t"))
+                nc.scalar.copy(out=dst, in_=bank[:].rearrange("p g u q -> p g q u"))
             else:
-                planes[i] = work.tile([P, 2, PACK, P], BF16, name="pl")
-                nc.vector.tensor_copy(out=planes[i][:], in_=bank[:])
-                nc.gpsimd.tensor_scalar(
-                    out=dst,
-                    in0=planes[i][:].rearrange("p g t q -> p g q t"),
-                    scalar1=1.0,
-                    scalar2=0.0,
-                    op0=ALU.mult,
-                    op1=ALU.add,
-                )
+                nc.vector.tensor_copy(out=dst, in_=bank[:].rearrange("p g u q -> p g q u"))
 
         def quantise_e(i):
             if not live(i):
@@ -217,7 +212,7 @@ def tile_dotattention_kernel(tc, query, key, value, out):
             nc.vector.quantize_mx(
                 out=e_codes[i][:].bitcast(FP8X4),
                 scales=e_scales[i][:],
-                in_=grouped[i][:].rearrange("p g q t -> p (g q t)"),
+                in_=grouped[i][:],
             )
 
         def e_times_value(i):

@@ -63,6 +63,7 @@ def tile_dotattention_kernel(tc, query, key, value, out):
         nc.scalar.activation(out=warm[:], in_=warm[:], func=ACT.Exp)
 
         kT, qT, v_grouped, v_codes, v_scales = {}, {}, {}, {}, {}
+        waiting = []
 
         def transpose_half(h, name, half):
             if h not in kT:
@@ -77,15 +78,31 @@ def tile_dotattention_kernel(tc, query, key, value, out):
                     rows = q_raw[h][:, n * D : (n + 1) * D]
                 nc.tensor.transpose(bank[:, a // PACK, a % PACK, :], rows, ident[:])
             cols = slice(half * HALF, (half + 1) * HALF)
-            if name == "key":
-                for a in range(2):
-                    c0 = half * HALF + a * BANK
-                    nc.vector.tensor_copy(
-                        out=kT[h][:, c0 : c0 + BANK].rearrange("d (u p e) -> d u p e", u=2, e=2),
-                        in_=bank[:, a].rearrange("d (u e) p -> d u p e", u=2),
-                    )
-            else:
+            if name == "query":
                 nc.scalar.copy(out=qT[h][:, cols], in_=bank[:].rearrange("p a b c -> p (a b c)"))
+            elif h == 0:
+                for a in range(2):
+                    nc.scalar.copy(out=key_columns(h, 2 * half + a), in_=bank[:, a].rearrange("d (u e) p -> d u p e", u=2))
+            else:
+                waiting.append((h, half, bank))
+
+        def key_columns(h, g):
+            return kT[h][:, g * BANK : (g + 1) * BANK].rearrange("d (u p e) -> d u p e", u=2, e=2)
+
+        def key_out():
+            for h, half, bank in waiting:
+                staged = work.tile([P, 2, PACK, P], BF16, name="ks")
+                nc.vector.tensor_copy(out=staged[:], in_=bank[:])
+                for a in range(2):
+                    nc.gpsimd.tensor_scalar(
+                        out=key_columns(h, 2 * half + a),
+                        in0=staged[:, a].rearrange("d (u e) p -> d u p e", u=2),
+                        scalar1=1.0,
+                        scalar2=0.0,
+                        op0=ALU.mult,
+                        op1=ALU.add,
+                    )
+            waiting.clear()
 
         def group_value(h, g):
             if g == 0:
@@ -267,6 +284,7 @@ def tile_dotattention_kernel(tc, query, key, value, out):
             score(p + 4, 1)
             exponential(p + 1)
             quantise_e(p - 1)
+            key_out()
             if p == -2:
                 quantise_value(0)
             if ahead and n == 12:

@@ -23,6 +23,7 @@ BANK = 512
 HALF = S // 2
 GROUP = 4
 NT = H * TILES
+FIRST = 4
 FLOPS = 2 * 2 * H * S * S * D
 
 
@@ -44,10 +45,17 @@ def tile_dotattention_kernel(tc, query, key, value, out):
         for h in range(H):
             kr = raw.tile([P, PASSES, PACK, D], BF16, name="kr")
             k_view = key[0, h].rearrange("(g p t) d -> p g t d", g=PASSES, t=PACK)
-            nc.sync.dma_start(out=kr[:, 0:2], in_=k_view[:, 0:2])
             qr = raw.tile([P, TILES * D], BF16, name="qr")
-            nc.sync.dma_start(out=qr[:], in_=query[0, h].rearrange("(p n) d -> p (n d)", n=TILES))
-            nc.sync.dma_start(out=kr[:, 2:4], in_=k_view[:, 2:4])
+            q_view = query[0, h].rearrange("(p n) d -> p (n d)", n=TILES)
+            if h == 0:
+                nc.sync.dma_start(out=kr[:, 0:1], in_=k_view[:, 0:1])
+                nc.sync.dma_start(out=qr[:, : FIRST * D], in_=q_view[:, : FIRST * D])
+                for g in range(1, PASSES):
+                    nc.sync.dma_start(out=kr[:, g : g + 1], in_=k_view[:, g : g + 1])
+                nc.sync.dma_start(out=qr[:, FIRST * D :], in_=q_view[:, FIRST * D :])
+            else:
+                nc.sync.dma_start(out=kr[:], in_=k_view)
+                nc.sync.dma_start(out=qr[:], in_=q_view)
             vr = raw.tile([P, PASSES, PACK, D], BF16, name="vr")
             nc.sync.dma_start(out=vr[:], in_=value[0, h].rearrange("(g p t) d -> p g t d", g=PASSES, t=PACK))
             k_raw.append(kr)
@@ -80,11 +88,24 @@ def tile_dotattention_kernel(tc, query, key, value, out):
             cols = slice(half * HALF, (half + 1) * HALF)
             if name == "query":
                 nc.scalar.copy(out=qT[h][:, cols], in_=bank[:].rearrange("p a b c -> p (a b c)"))
-            elif h == 0:
-                for a in range(2):
-                    nc.scalar.copy(out=key_columns(h, 2 * half + a), in_=bank[:, a].rearrange("d (u e) p -> d u p e", u=2))
             else:
                 waiting.append((h, half, bank))
+
+        def first_key(g, engine):
+            bank = ps_t.tile([P, PACK, P], BF16, name="tb")
+            for t in range(PACK):
+                nc.tensor.transpose(bank[:, t, :], k_raw[0][:, g, t, :], ident[:])
+            stepped = bank[:].rearrange("d (u e) p -> d u p e", u=2)
+            if engine == "vector":
+                nc.vector.tensor_copy(out=key_columns(0, g), in_=stepped)
+            else:
+                nc.scalar.copy(out=key_columns(0, g), in_=stepped)
+
+        def first_query(n0, count):
+            bank = ps_t.tile([P, count, P], BF16, name="tb")
+            for a in range(count):
+                nc.tensor.transpose(bank[:, a, :], q_raw[0][:, (n0 + a) * D : (n0 + a + 1) * D], ident[:])
+            nc.scalar.copy(out=qT[0][:, n0 * P : (n0 + count) * P], in_=bank[:].rearrange("p a c -> p (a c)"))
 
         def key_columns(h, g):
             return kT[h][:, g * BANK : (g + 1) * BANK].rearrange("d (u p e) -> d u p e", u=2, e=2)
@@ -132,8 +153,10 @@ def tile_dotattention_kernel(tc, query, key, value, out):
             return 0 <= i < NT
 
         def route(i):
-            if i >= NT - 3:
-                return ("vector", "scalar" if i == NT - 1 else "vector")
+            if i == NT - 2:
+                return ("vector", "vector")
+            if i == NT - 1:
+                return ("vector", "scalar")
             return ("scalar", "scalar")
 
         def score(i, j):
@@ -267,11 +290,15 @@ def tile_dotattention_kernel(tc, query, key, value, out):
                 out=out[0, h].rearrange("(p n) d -> p n d", n=TILES)[:, n - GROUP + 1 : n + 1, :], in_=result[:]
             )
 
-        transpose_half(0, "key", 0)
-        transpose_half(0, "query", 0)
+        kT[0] = keep.tile([P, S], BF16, name="kt")
+        qT[0] = keep.tile([P, S], BF16, name="qt")
+        first_key(0, "vector")
+        first_query(0, FIRST)
+        first_key(1, "scalar")
         score(0, 0)
+        first_key(2, "scalar")
         score(0, 1)
-        transpose_half(0, "key", 1)
+        first_key(3, "scalar")
         for p in range(-3, NT + 3):
             h, n = divmod(p, TILES)
             ahead = 0 <= h < H - 1
@@ -285,14 +312,14 @@ def tile_dotattention_kernel(tc, query, key, value, out):
             exponential(p + 1)
             quantise_e(p - 1)
             key_out()
-            if p == -2:
+            if p == 1:
                 quantise_value(0)
             if ahead and n == 12:
                 quantise_value(h + 1)
             planes_out(p, 0)
-            if p == -3:
-                for g in range(PASSES):
-                    group_value(0, g)
+            if p in (-2, -1):
+                group_value(0, 2 * (p + 2))
+                group_value(0, 2 * (p + 2) + 1)
             if ahead and 8 <= n < 8 + PASSES:
                 group_value(h + 1, n - 8)
             transpose_e(p + 1, 0)
@@ -302,6 +329,8 @@ def tile_dotattention_kernel(tc, query, key, value, out):
             transpose_e(p + 1, 1)
             normalise_and_store(p - 2)
             if p == -3:
-                transpose_half(0, "query", 1)
+                first_query(FIRST, 8)
+            if p == -2:
+                first_query(FIRST + 8, TILES - FIRST - 8)
             if ahead and n % 2 == 1 and n < 8:
                 transpose_half(h + 1, "key" if n < 4 else "query", (n // 2) % 2)

@@ -85,11 +85,7 @@ def tile_dotattention_kernel(tc, query, key, value, out):
                     n = 2 * PACK * half + a
                     rows = q_raw[h][:, n * D : (n + 1) * D]
                 nc.tensor.transpose(bank[:, a // PACK, a % PACK, :], rows, ident[:])
-            cols = slice(half * HALF, (half + 1) * HALF)
-            if name == "query":
-                nc.scalar.copy(out=qT[h][:, cols], in_=bank[:].rearrange("p a b c -> p (a b c)"))
-            else:
-                waiting.append((h, half, bank))
+            waiting.append((h, name, half, bank))
 
         def first_key(g, engine):
             bank = ps_t.tile([P, PACK, P], BF16, name="tb")
@@ -111,7 +107,11 @@ def tile_dotattention_kernel(tc, query, key, value, out):
             return kT[h][:, g * BANK : (g + 1) * BANK].rearrange("d (u p e) -> d u p e", u=2, e=2)
 
         def key_out():
-            for h, half, bank in waiting:
+            for h, name, half, bank in waiting:
+                if name == "query":
+                    cols = slice(half * HALF, (half + 1) * HALF)
+                    nc.scalar.copy(out=qT[h][:, cols], in_=bank[:].rearrange("p a b c -> p (a b c)"))
+                    continue
                 staged = work.tile([P, 2, PACK, P], BF16, name="ks")
                 nc.vector.tensor_copy(out=staged[:], in_=bank[:])
                 for a in range(2):

@@ -113,7 +113,7 @@ def tile_dotattention_kernel(tc, query, key, value, out):
                     nc.scalar.copy(out=qT[h][:, cols], in_=bank[:].rearrange("p a b c -> p (a b c)"))
                     continue
                 staged = work.tile([P, 2, PACK, P], BF16, name="ks")
-                nc.vector.tensor_copy(out=staged[:], in_=bank[:])
+                nc.scalar.copy(out=staged[:], in_=bank[:])
                 for a in range(2):
                     nc.gpsimd.tensor_scalar(
                         out=key_columns(h, 2 * half + a),

@@ -42,6 +42,12 @@ def tile_dotattention_kernel(tc, query, key, value, out):
         ctx.enter_context(tc.manual_schedule())
 
         q_raw, k_raw, v_raw = [], [], []
+
+        def load_value(h):
+            vr = raw.tile([P, PASSES, PACK, D], BF16, name="vr")
+            nc.sync.dma_start(out=vr[:], in_=value[0, h].rearrange("(g p t) d -> p g t d", g=PASSES, t=PACK))
+            v_raw.append(vr)
+
         for h in range(H):
             kr = raw.tile([P, PASSES, PACK, D], BF16, name="kr")
             k_view = key[0, h].rearrange("(g p t) d -> p g t d", g=PASSES, t=PACK)
@@ -55,12 +61,12 @@ def tile_dotattention_kernel(tc, query, key, value, out):
                 nc.sync.dma_start(out=qr[:, FIRST * D :], in_=q_view[:, FIRST * D :])
             else:
                 nc.sync.dma_start(out=kr[:], in_=k_view)
+                if h == 1:
+                    load_value(0)
                 nc.sync.dma_start(out=qr[:], in_=q_view)
-            vr = raw.tile([P, PASSES, PACK, D], BF16, name="vr")
-            nc.sync.dma_start(out=vr[:], in_=value[0, h].rearrange("(g p t) d -> p g t d", g=PASSES, t=PACK))
+                load_value(h)
             k_raw.append(kr)
             q_raw.append(qr)
-            v_raw.append(vr)
 
         ident = const.tile([P, P], BF16)
         make_identity(nc, ident[:])
@@ -71,7 +77,7 @@ def tile_dotattention_kernel(tc, query, key, value, out):
         nc.scalar.activation(out=warm[:], in_=warm[:], func=ACT.Exp)
 
         kT, qT, v_grouped, v_codes, v_scales = {}, {}, {}, {}, {}
-        waiting = []
+        waiting, unordered = [], []
 
         def transpose_half(h, name, half):
             if h not in kT:
@@ -101,6 +107,9 @@ def tile_dotattention_kernel(tc, query, key, value, out):
             bank = ps_t.tile([P, count, P], BF16, name="tb")
             for a in range(count):
                 nc.tensor.transpose(bank[:, a, :], q_raw[0][:, (n0 + a) * D : (n0 + a + 1) * D], ident[:])
+            if n0 + count == TILES:
+                waiting.append((0, "first query", n0, bank))
+                return
             nc.scalar.copy(out=qT[0][:, n0 * P : (n0 + count) * P], in_=bank[:].rearrange("p a c -> p (a c)"))
 
         def key_columns(h, g):
@@ -108,12 +117,20 @@ def tile_dotattention_kernel(tc, query, key, value, out):
 
         def key_out():
             for h, name, half, bank in waiting:
+                if name == "first query":
+                    nc.scalar.copy(out=qT[h][:, half * P :], in_=bank[:].rearrange("p a c -> p (a c)"))
+                    continue
                 if name == "query":
                     cols = slice(half * HALF, (half + 1) * HALF)
                     nc.scalar.copy(out=qT[h][:, cols], in_=bank[:].rearrange("p a b c -> p (a b c)"))
                     continue
                 staged = work.tile([P, 2, PACK, P], BF16, name="ks")
                 nc.scalar.copy(out=staged[:], in_=bank[:])
+                unordered.append((h, half, staged))
+            waiting.clear()
+
+        def order_key():
+            for h, half, staged in unordered:
                 for a in range(2):
                     nc.gpsimd.tensor_scalar(
                         out=key_columns(h, 2 * half + a),
@@ -123,7 +140,7 @@ def tile_dotattention_kernel(tc, query, key, value, out):
                         op0=ALU.mult,
                         op1=ALU.add,
                     )
-            waiting.clear()
+            unordered.clear()
 
         def group_value(h, g):
             if g == 0:
@@ -304,6 +321,9 @@ def tile_dotattention_kernel(tc, query, key, value, out):
             ahead = 0 <= h < H - 1
             score(p + 3, 2)
             score(p + 3, 3)
+            if p == -3:
+                transpose_half(1, "key", 0)
+                key_out()
             e_times_value(p - 2)
             score_out(p + 3, 0)
             score(p + 4, 0)
@@ -312,6 +332,8 @@ def tile_dotattention_kernel(tc, query, key, value, out):
             exponential(p + 1)
             quantise_e(p - 1)
             key_out()
+            if p >= 0:
+                order_key()
             if p == 1:
                 quantise_value(0)
             if ahead and n == 12:
@@ -330,7 +352,9 @@ def tile_dotattention_kernel(tc, query, key, value, out):
             normalise_and_store(p - 2)
             if p == -3:
                 first_query(FIRST, 8)
-            if p == -2:
+                transpose_half(1, "key", 1)
+                key_out()
+            if p == 0:
                 first_query(FIRST + 8, TILES - FIRST - 8)
-            if ahead and n % 2 == 1 and n < 8:
+            if ahead and n % 2 == 1 and n < 8 and (h > 0 or n > 3):
                 transpose_half(h + 1, "key" if n < 4 else "query", (n // 2) % 2)

@@ -23,7 +23,9 @@ BANK = 512
 HALF = S // 2
 GROUP = 4
 NT = H * TILES
+LAST = NT - 1
 FIRST = 4
+WARM_UP = 12
 FLOPS = 2 * 2 * H * S * S * D
 
 
@@ -75,6 +77,12 @@ def tile_dotattention_kernel(tc, query, key, value, out):
         warm = const.tile([P, 1], F32)
         nc.vector.memset(warm[:], 0.0)
         nc.scalar.activation(out=warm[:], in_=warm[:], func=ACT.Exp)
+
+        zeros = const.tile([P, P], BF16)
+        nc.vector.memset(zeros[:], 0.0)
+        unread = ps_t.tile([P, P], F32, name="tb")
+        for step in range(WARM_UP):
+            nc.tensor.matmul(out=unread[:], lhsT=zeros[:], rhs=zeros[:], start=True, stop=True)
 
         kT, qT, v_grouped, v_codes, v_scales = {}, {}, {}, {}, {}
         waiting, unordered = [], []
@@ -169,13 +177,6 @@ def tile_dotattention_kernel(tc, query, key, value, out):
         def live(i):
             return 0 <= i < NT
 
-        def route(i):
-            if i == NT - 2:
-                return ("vector", "vector")
-            if i == NT - 1:
-                return ("vector", "scalar")
-            return ("scalar", "scalar")
-
         def score(i, j):
             if not live(i):
                 return
@@ -246,20 +247,23 @@ def tile_dotattention_kernel(tc, query, key, value, out):
             if half == 0:
                 grouped[i] = work.tile([P, S], BF16, name="grp", align_bytes=64)
             words = e_bf16[i][:].bitcast(F32)
+            side_by_side = bank[:].rearrange("p g u q -> p g (u q)").rearrange("p g (q u) -> p g q u", u=2)
             for a in range(4):
                 c = 4 * half + a
-                nc.tensor.transpose(bank[:, a // 2, a % 2, :], words[:, c * P : (c + 1) * P], ident_words[:])
+                out = side_by_side[:, a // 2, :, a % 2] if i == LAST - 1 else bank[:, a // 2, a % 2, :]
+                nc.tensor.transpose(out, words[:, c * P : (c + 1) * P], ident_words[:])
 
         def planes_out(i, half):
             if not live(i):
                 return
-            way = route(i)[half]
             bank = plane_bank[(i, half)]
-            dst = grouped[i][:, half * HALF : (half + 1) * HALF].bitcast(F32).rearrange("p (g q u) -> p g q u", g=2, u=2)
-            if way == "scalar":
-                nc.scalar.copy(out=dst, in_=bank[:].rearrange("p g u q -> p g q u"))
+            dst = grouped[i][:, half * HALF : (half + 1) * HALF].bitcast(F32)
+            if i == LAST - 1:
+                nc.vector.tensor_copy(out=dst, in_=bank[:].rearrange("p g u q -> p (g u q)"))
             else:
-                nc.vector.tensor_copy(out=dst, in_=bank[:].rearrange("p g u q -> p g q u"))
+                nc.scalar.copy(
+                    out=dst.rearrange("p (g q u) -> p g q u", g=2, u=2), in_=bank[:].rearrange("p g u q -> p g q u")
+                )
 
         def quantise_e(i):
             if not live(i):
@@ -307,16 +311,103 @@ def tile_dotattention_kernel(tc, query, key, value, out):
                 out=out[0, h].rearrange("(p n) d -> p n d", n=TILES)[:, n - GROUP + 1 : n + 1, :], in_=result[:]
             )
 
+        last = {}
+
+        def last_exponential(half):
+            cols = slice(half * HALF, (half + 1) * HALF)
+            if half == 0:
+                e_bf16[LAST] = work.tile([P, S], BF16, name="e")
+                last["sums"] = small.tile([P, 2], F32, name="hs")
+            nc.scalar.activation(
+                out=e_bf16[LAST][:, cols],
+                in_=neg_score[LAST][:, cols],
+                func=ACT.Exp,
+                bias=neg_max[LAST][:, 0:1],
+                scale=-1.0,
+                accum_out=last["sums"][:, half : half + 1],
+            )
+            if half == 1:
+                nc.gpsimd.tensor_scalar(
+                    out=row_sum[LAST // GROUP][:, GROUP - 1 : GROUP],
+                    in0=last["sums"][:, 0:1],
+                    scalar1=last["sums"][:, 1:2],
+                    scalar2=1.0,
+                    op0=ALU.add,
+                    op1=ALU.mult,
+                )
+
+        def last_transpose(g):
+            if g == 0:
+                grouped[LAST] = work.tile([P, S], BF16, name="grp", align_bytes=64)
+            bank = ps_s.tile([P, P, 2], F32, name="s")
+            last[g] = bank
+            words = e_bf16[LAST][:].bitcast(F32)
+            for u in range(2):
+                c = 2 * g + u
+                nc.tensor.transpose(bank[:, :, u], words[:, c * P : (c + 1) * P], ident_words[:])
+
+        def last_planes_out(g, engine):
+            dst = grouped[LAST][:, g * BANK : (g + 1) * BANK].bitcast(F32)
+            src = last[g][:].rearrange("p q u -> p (q u)")
+            if engine == "vector":
+                nc.vector.tensor_copy(out=dst, in_=src)
+            else:
+                nc.scalar.copy(out=dst, in_=src)
+
+        def last_quantise(half):
+            if half == 0:
+                e_codes[LAST] = work.tile([P, PASSES * P], U32, name="ec", align_bytes=64)
+                e_scales[LAST] = work.tile([P, PASSES * P], U8, name="es", align_bytes=64)
+            cols = slice(half * 2 * P, (half + 1) * 2 * P)
+            nc.vector.quantize_mx(
+                out=e_codes[LAST][:, cols].bitcast(FP8X4),
+                scales=e_scales[LAST][:, cols],
+                in_=grouped[LAST][:, half * HALF : (half + 1) * HALF],
+            )
+
+        def last_e_times_value(g):
+            if g == 0:
+                last["out"] = ps_s.tile([P, D], F32, name="s")
+            cols = slice(g * P, (g + 1) * P)
+            nc.tensor.matmul_mx(
+                out=last["out"][:],
+                lhsT=e_codes[LAST][:, cols].bitcast(FP8X4),
+                lhsT_scale=e_scales[LAST][:, cols],
+                rhs=v_codes[H - 1][:, cols].bitcast(FP8X4),
+                rhs_scale=v_scales[H - 1][:, cols],
+                start=(g == 0),
+                stop=(g == PASSES - 1),
+            )
+
+        def last_group_out():
+            view = out[0, H - 1].rearrange("(p n) d -> p n d", n=TILES)
+            inverse = small.tile([P, GROUP], F32, name="rc")
+            nc.vector.reciprocal(out=inverse[:], in_=row_sum[LAST // GROUP][:])
+            three = small.tile([P, GROUP - 1, D], F32, name="ob")
+            nc.vector.tensor_tensor(
+                out=three[:],
+                in0=out_bank[LAST // GROUP][:, : GROUP - 1, :],
+                in1=inverse[:, : GROUP - 1].unsqueeze(2).to_broadcast([P, GROUP - 1, D]),
+                op=ALU.mult,
+            )
+            nc.sync.dma_start(out=view[:, TILES - GROUP : TILES - 1, :], in_=three[:])
+            one = small.tile([P, D], F32, name="ol")
+            nc.vector.tensor_scalar(
+                out=one[:], in0=last["out"][:], scalar1=inverse[:, GROUP - 1 : GROUP], scalar2=None, op0=ALU.mult
+            )
+            nc.sync.dma_start(out=view[:, TILES - 1, :], in_=one[:])
+
         kT[0] = keep.tile([P, S], BF16, name="kt")
         qT[0] = keep.tile([P, S], BF16, name="qt")
         first_key(0, "vector")
-        first_query(0, FIRST)
-        first_key(1, "scalar")
+        first_query(0, 1)
+        first_key(1, "vector")
         score(0, 0)
         first_key(2, "scalar")
         score(0, 1)
+        first_query(1, FIRST - 1)
         first_key(3, "scalar")
-        for p in range(-3, NT + 3):
+        for p in range(-3, LAST - 1):
             h, n = divmod(p, TILES)
             ahead = 0 <= h < H - 1
             score(p + 3, 2)
@@ -358,3 +449,25 @@ def tile_dotattention_kernel(tc, query, key, value, out):
                 first_query(FIRST + 8, TILES - FIRST - 8)
             if ahead and n % 2 == 1 and n < 8 and (h > 0 or n > 3):
                 transpose_half(h + 1, "key" if n < 4 else "query", (n // 2) % 2)
+        e_times_value(LAST - 3)
+        last_exponential(0)
+        last_exponential(1)
+        quantise_e(LAST - 2)
+        planes_out(LAST - 1, 0)
+        last_transpose(0)
+        last_transpose(1)
+        planes_out(LAST - 1, 1)
+        e_times_value(LAST - 2)
+        quantise_e(LAST - 1)
+        last_planes_out(0, "vector")
+        last_planes_out(1, "vector")
+        last_quantise(0)
+        last_transpose(2)
+        last_transpose(3)
+        e_times_value(LAST - 1)
+        last_planes_out(2, "vector")
+        last_planes_out(3, "scalar")
+        last_quantise(1)
+        for g in range(PASSES):
+            last_e_times_value(g)
+        last_group_out()

@@ -134,21 +134,21 @@ def tile_dotattention_kernel(tc, query, key, value, out):
                     continue
                 staged = work.tile([P, 2, PACK, P], BF16, name="ks")
                 nc.scalar.copy(out=staged[:], in_=bank[:])
-                unordered.append((h, half, staged))
+                unordered.extend((h, 2 * half + a, staged) for a in range(2))
             waiting.clear()
 
         def order_key():
-            for h, half, staged in unordered:
-                for a in range(2):
-                    nc.gpsimd.tensor_scalar(
-                        out=key_columns(h, 2 * half + a),
-                        in0=staged[:, a].rearrange("d (u e) p -> d u p e", u=2),
-                        scalar1=1.0,
-                        scalar2=0.0,
-                        op0=ALU.mult,
-                        op1=ALU.add,
-                    )
-            unordered.clear()
+            if unordered:
+                h, g, staged = unordered[0]
+                unordered.remove(unordered[0])
+                nc.gpsimd.tensor_scalar(
+                    out=key_columns(h, g),
+                    in0=staged[:, g % 2].rearrange("d (u e) p -> d u p e", u=2),
+                    scalar1=1.0,
+                    scalar2=0.0,
+                    op0=ALU.mult,
+                    op1=ALU.add,
+                )
 
         def group_value(h, g):
             if g == 0:
@@ -423,8 +423,6 @@ def tile_dotattention_kernel(tc, query, key, value, out):
             exponential(p + 1)
             quantise_e(p - 1)
             key_out()
-            if p >= 0:
-                order_key()
             if p == 1:
                 quantise_value(0)
             if ahead and n == 12:
@@ -438,6 +436,8 @@ def tile_dotattention_kernel(tc, query, key, value, out):
             transpose_e(p + 1, 0)
             score_out(p + 3, 2)
             score_out(p + 3, 3)
+            if p >= 0:
+                order_key()
             planes_out(p, 1)
             transpose_e(p + 1, 1)
             normalise_and_store(p - 2)

@@ -133,7 +133,10 @@ def tile_dotattention_kernel(tc, query, key, value, out):
                     nc.scalar.copy(out=qT[h][:, cols], in_=bank[:].rearrange("p a b c -> p (a b c)"))
                     continue
                 staged = work.tile([P, 2, PACK, P], BF16, name="ks")
-                nc.scalar.copy(out=staged[:], in_=bank[:])
+                if h >= 2:
+                    nc.vector.tensor_copy(out=staged[:], in_=bank[:])
+                else:
+                    nc.scalar.copy(out=staged[:], in_=bank[:])
                 unordered.extend((h, 2 * half + a, staged) for a in range(2))
             waiting.clear()
 
@@ -244,8 +247,8 @@ def tile_dotattention_kernel(tc, query, key, value, out):
                 return
             bank = ps_t.tile([P, 2, 2, P], F32, name="tb")
             plane_bank[(i, half)] = bank
-            if half == 0:
-                grouped[i] = work.tile([P, S], BF16, name="grp", align_bytes=64)
+            if half == 0 and i % 2 == 0:
+                grouped[i // 2] = work.tile([P, 2 * S], BF16, name="grp", align_bytes=64)
             words = e_bf16[i][:].bitcast(F32)
             side_by_side = bank[:].rearrange("p g u q -> p g (u q)").rearrange("p g (q u) -> p g q u", u=2)
             for a in range(4):
@@ -257,7 +260,8 @@ def tile_dotattention_kernel(tc, query, key, value, out):
             if not live(i):
                 return
             bank = plane_bank[(i, half)]
-            dst = grouped[i][:, half * HALF : (half + 1) * HALF].bitcast(F32)
+            start = i % 2 * S + half * HALF
+            dst = grouped[i // 2][:, start : start + HALF].bitcast(F32)
             if i == LAST - 1:
                 nc.vector.tensor_copy(out=dst, in_=bank[:].rearrange("p g u q -> p (g u q)"))
             else:
@@ -265,15 +269,18 @@ def tile_dotattention_kernel(tc, query, key, value, out):
                     out=dst.rearrange("p (g q u) -> p g q u", g=2, u=2), in_=bank[:].rearrange("p g u q -> p g q u")
                 )
 
-        def quantise_e(i):
+        def quantise_e(i, tiles):
             if not live(i):
                 return
-            e_codes[i] = work.tile([P, PASSES * P], U32, name="ec", align_bytes=64)
-            e_scales[i] = work.tile([P, PASSES * P], U8, name="es", align_bytes=64)
+            pair, place = divmod(i, 2)
+            if place == 0:
+                e_codes[pair] = work.tile([P, 2 * PASSES * P], U32, name="ec", align_bytes=64)
+                e_scales[pair] = work.tile([P, 2 * PASSES * P], U8, name="es", align_bytes=64)
+            words = slice(place * PASSES * P, (place + tiles) * PASSES * P)
             nc.vector.quantize_mx(
-                out=e_codes[i][:].bitcast(FP8X4),
-                scales=e_scales[i][:],
-                in_=grouped[i][:],
+                out=e_codes[pair][:, words].bitcast(FP8X4),
+                scales=e_scales[pair][:, words],
+                in_=grouped[pair][:, place * S : (place + tiles) * S],
             )
 
         def e_times_value(i):
@@ -284,10 +291,11 @@ def tile_dotattention_kernel(tc, query, key, value, out):
                 out_bank[i // GROUP] = ps_o.tile([P, GROUP, D], F32, name="o")
             for g in range(PASSES):
                 cols = slice(g * P, (g + 1) * P)
+                e_cols = slice((i % 2 * PASSES + g) * P, (i % 2 * PASSES + g + 1) * P)
                 nc.tensor.matmul_mx(
                     out=out_bank[i // GROUP][:, i % GROUP, :],
-                    lhsT=e_codes[i][:, cols].bitcast(FP8X4),
-                    lhsT_scale=e_scales[i][:, cols],
+                    lhsT=e_codes[i // 2][:, e_cols].bitcast(FP8X4),
+                    lhsT_scale=e_scales[i // 2][:, e_cols],
                     rhs=v_codes[h][:, cols].bitcast(FP8X4),
                     rhs_scale=v_scales[h][:, cols],
                     start=(g == 0),
@@ -338,7 +346,7 @@ def tile_dotattention_kernel(tc, query, key, value, out):
 
         def last_transpose(g):
             if g == 0:
-                grouped[LAST] = work.tile([P, S], BF16, name="grp", align_bytes=64)
+                last["grouped"] = work.tile([P, S], BF16, name="grp", align_bytes=64)
             bank = ps_s.tile([P, P, 2], F32, name="s")
             last[g] = bank
             words = e_bf16[LAST][:].bitcast(F32)
@@ -347,7 +355,7 @@ def tile_dotattention_kernel(tc, query, key, value, out):
                 nc.tensor.transpose(bank[:, :, u], words[:, c * P : (c + 1) * P], ident_words[:])
 
         def last_planes_out(g, engine):
-            dst = grouped[LAST][:, g * BANK : (g + 1) * BANK].bitcast(F32)
+            dst = last["grouped"][:, g * BANK : (g + 1) * BANK].bitcast(F32)
             src = last[g][:].rearrange("p q u -> p (q u)")
             if engine == "vector":
                 nc.vector.tensor_copy(out=dst, in_=src)
@@ -356,13 +364,13 @@ def tile_dotattention_kernel(tc, query, key, value, out):
 
         def last_quantise(half):
             if half == 0:
-                e_codes[LAST] = work.tile([P, PASSES * P], U32, name="ec", align_bytes=64)
-                e_scales[LAST] = work.tile([P, PASSES * P], U8, name="es", align_bytes=64)
+                last["codes"] = work.tile([P, PASSES * P], U32, name="ec", align_bytes=64)
+                last["scales"] = work.tile([P, PASSES * P], U8, name="es", align_bytes=64)
             cols = slice(half * 2 * P, (half + 1) * 2 * P)
             nc.vector.quantize_mx(
-                out=e_codes[LAST][:, cols].bitcast(FP8X4),
-                scales=e_scales[LAST][:, cols],
-                in_=grouped[LAST][:, half * HALF : (half + 1) * HALF],
+                out=last["codes"][:, cols].bitcast(FP8X4),
+                scales=last["scales"][:, cols],
+                in_=last["grouped"][:, half * HALF : (half + 1) * HALF],
             )
 
         def last_e_times_value(g):
@@ -371,8 +379,8 @@ def tile_dotattention_kernel(tc, query, key, value, out):
             cols = slice(g * P, (g + 1) * P)
             nc.tensor.matmul_mx(
                 out=last["out"][:],
-                lhsT=e_codes[LAST][:, cols].bitcast(FP8X4),
-                lhsT_scale=e_scales[LAST][:, cols],
+                lhsT=last["codes"][:, cols].bitcast(FP8X4),
+                lhsT_scale=last["scales"][:, cols],
                 rhs=v_codes[H - 1][:, cols].bitcast(FP8X4),
                 rhs_scale=v_scales[H - 1][:, cols],
                 start=(g == 0),
@@ -413,15 +421,19 @@ def tile_dotattention_kernel(tc, query, key, value, out):
             score(p + 3, 2)
             score(p + 3, 3)
             if p == -3:
-                transpose_half(1, "key", 0)
-                key_out()
-            e_times_value(p - 2)
+                first_query(FIRST, 8)
+            if p % 2 == 1:
+                e_times_value(p - 3)
+                e_times_value(p - 2)
             score_out(p + 3, 0)
             score(p + 4, 0)
             score_out(p + 3, 1)
             score(p + 4, 1)
             exponential(p + 1)
-            quantise_e(p - 1)
+            if p == LAST - 2:
+                quantise_e(p - 1, 1)
+            elif p % 2 == 0:
+                quantise_e(p - 2, 2)
             key_out()
             if p == 1:
                 quantise_value(0)
@@ -442,23 +454,22 @@ def tile_dotattention_kernel(tc, query, key, value, out):
             transpose_e(p + 1, 1)
             normalise_and_store(p - 2)
             if p == -3:
-                first_query(FIRST, 8)
-                transpose_half(1, "key", 1)
+                transpose_half(1, "key", 0)
                 key_out()
             if p == 0:
                 first_query(FIRST + 8, TILES - FIRST - 8)
-            if ahead and n % 2 == 1 and n < 8 and (h > 0 or n > 3):
+            if ahead and n % 2 == 1 and n < 8 and (h > 0 or n > 1):
                 transpose_half(h + 1, "key" if n < 4 else "query", (n // 2) % 2)
         e_times_value(LAST - 3)
         last_exponential(0)
         last_exponential(1)
-        quantise_e(LAST - 2)
+        quantise_e(LAST - 2, 1)
         planes_out(LAST - 1, 0)
         last_transpose(0)
         last_transpose(1)
         planes_out(LAST - 1, 1)
         e_times_value(LAST - 2)
-        quantise_e(LAST - 1)
+        quantise_e(LAST - 1, 1)
         last_planes_out(0, "vector")
         last_planes_out(1, "vector")
         last_quantise(0)

@@ -78,6 +78,8 @@ def tile_dotattention_kernel(tc, query, key, value, out):
         nc.vector.memset(warm[:], 0.0)
         nc.scalar.activation(out=warm[:], in_=warm[:], func=ACT.Exp)
 
+        minus_one = const.tile([P, GROUP], F32)
+        nc.gpsimd.memset(minus_one[:], -1.0)
         zeros = const.tile([P, P], BF16)
         nc.vector.memset(zeros[:], 0.0)
         unread = ps_t.tile([P, P], F32, name="tb")
@@ -175,7 +177,7 @@ def tile_dotattention_kernel(tc, query, key, value, out):
             )
 
         score_bank, neg_score, bank_min, neg_max, row_sum, e_bf16 = {}, {}, {}, {}, {}, {}
-        plane_bank, planes, grouped, e_codes, e_scales, out_bank = {}, {}, {}, {}, {}, {}
+        plane_bank, inverse, grouped, e_codes, e_scales, out_bank = {}, {}, {}, {}, {}, {}
 
         def live(i):
             return 0 <= i < NT
@@ -253,7 +255,7 @@ def tile_dotattention_kernel(tc, query, key, value, out):
             side_by_side = bank[:].rearrange("p g u q -> p g (u q)").rearrange("p g (q u) -> p g q u", u=2)
             for a in range(4):
                 c = 4 * half + a
-                out = side_by_side[:, a // 2, :, a % 2] if i == LAST - 1 else bank[:, a // 2, a % 2, :]
+                out = side_by_side[:, a // 2, :, a % 2] if i >= LAST - 2 else bank[:, a // 2, a % 2, :]
                 nc.tensor.transpose(out, words[:, c * P : (c + 1) * P], ident_words[:])
 
         def planes_out(i, half):
@@ -262,7 +264,7 @@ def tile_dotattention_kernel(tc, query, key, value, out):
             bank = plane_bank[(i, half)]
             start = i % 2 * S + half * HALF
             dst = grouped[i // 2][:, start : start + HALF].bitcast(F32)
-            if i == LAST - 1:
+            if i >= LAST - 2:
                 nc.vector.tensor_copy(out=dst, in_=bank[:].rearrange("p g u q -> p (g u q)"))
             else:
                 nc.scalar.copy(
@@ -302,17 +304,21 @@ def tile_dotattention_kernel(tc, query, key, value, out):
                     stop=(g == PASSES - 1),
                 )
 
+        def invert_sums(group):
+            inverse[group] = small.tile([P, GROUP], F32, name="rc")
+            nc.gpsimd.tensor_tensor(
+                out=inverse[group][:], in0=row_sum[group][:], in1=minus_one[:], op=ALU.pow
+            )
+
         def normalise_and_store(i):
             if not live(i) or i % GROUP != GROUP - 1:
                 return
             h, n = divmod(i, TILES)
-            inverse = small.tile([P, GROUP], F32, name="rc")
-            nc.vector.reciprocal(out=inverse[:], in_=row_sum[i // GROUP][:])
             result = small.tile([P, GROUP, D], F32, name="ob")
             nc.vector.tensor_tensor(
                 out=result[:],
                 in0=out_bank[i // GROUP][:],
-                in1=inverse[:].unsqueeze(2).to_broadcast([P, GROUP, D]),
+                in1=inverse[i // GROUP][:].unsqueeze(2).to_broadcast([P, GROUP, D]),
                 op=ALU.mult,
             )
             nc.sync.dma_start(
@@ -389,19 +395,19 @@ def tile_dotattention_kernel(tc, query, key, value, out):
 
         def last_group_out():
             view = out[0, H - 1].rearrange("(p n) d -> p n d", n=TILES)
-            inverse = small.tile([P, GROUP], F32, name="rc")
-            nc.vector.reciprocal(out=inverse[:], in_=row_sum[LAST // GROUP][:])
+            last_inverse = small.tile([P, GROUP], F32, name="rc")
+            nc.vector.reciprocal(out=last_inverse[:], in_=row_sum[LAST // GROUP][:])
             three = small.tile([P, GROUP - 1, D], F32, name="ob")
             nc.vector.tensor_tensor(
                 out=three[:],
                 in0=out_bank[LAST // GROUP][:, : GROUP - 1, :],
-                in1=inverse[:, : GROUP - 1].unsqueeze(2).to_broadcast([P, GROUP - 1, D]),
+                in1=last_inverse[:, : GROUP - 1].unsqueeze(2).to_broadcast([P, GROUP - 1, D]),
                 op=ALU.mult,
             )
             nc.sync.dma_start(out=view[:, TILES - GROUP : TILES - 1, :], in_=three[:])
             one = small.tile([P, D], F32, name="ol")
             nc.vector.tensor_scalar(
-                out=one[:], in0=last["out"][:], scalar1=inverse[:, GROUP - 1 : GROUP], scalar2=None, op0=ALU.mult
+                out=one[:], in0=last["out"][:], scalar1=last_inverse[:, GROUP - 1 : GROUP], scalar2=None, op0=ALU.mult
             )
             nc.sync.dma_start(out=view[:, TILES - 1, :], in_=one[:])
 
@@ -450,6 +456,8 @@ def tile_dotattention_kernel(tc, query, key, value, out):
             score_out(p + 3, 3)
             if p >= 0:
                 order_key()
+            if p >= 0 and p % GROUP == GROUP - 1:
+                invert_sums(p // GROUP)
             planes_out(p, 1)
             transpose_e(p + 1, 1)
             normalise_and_store(p - 2)

@@ -393,10 +393,13 @@ def tile_dotattention_kernel(tc, query, key, value, out):
                 stop=(g == PASSES - 1),
             )
 
+        def last_invert():
+            last["inverse"] = small.tile([P, GROUP], F32, name="rc")
+            nc.vector.reciprocal(out=last["inverse"][:], in_=row_sum[LAST // GROUP][:])
+
         def last_group_out():
             view = out[0, H - 1].rearrange("(p n) d -> p n d", n=TILES)
-            last_inverse = small.tile([P, GROUP], F32, name="rc")
-            nc.vector.reciprocal(out=last_inverse[:], in_=row_sum[LAST // GROUP][:])
+            last_inverse = last["inverse"]
             three = small.tile([P, GROUP - 1, D], F32, name="ob")
             nc.vector.tensor_tensor(
                 out=three[:],
@@ -477,15 +480,16 @@ def tile_dotattention_kernel(tc, query, key, value, out):
         last_transpose(1)
         planes_out(LAST - 1, 1)
         e_times_value(LAST - 2)
-        quantise_e(LAST - 1, 1)
         last_planes_out(0, "vector")
         last_planes_out(1, "vector")
+        quantise_e(LAST - 1, 1)
         last_quantise(0)
         last_transpose(2)
         last_transpose(3)
         e_times_value(LAST - 1)
         last_planes_out(2, "vector")
         last_planes_out(3, "scalar")
+        last_invert()
         last_quantise(1)
         for g in range(PASSES):
             last_e_times_value(g)

@@ -182,6 +182,9 @@ def tile_dotattention_kernel(tc, query, key, value, out):
         def live(i):
             return 0 <= i < NT
 
+        def by_vector(i, half):
+            return 2 * i + half >= 2 * (LAST - 3) + 1
+
         def score(i, j):
             if not live(i):
                 return
@@ -255,7 +258,7 @@ def tile_dotattention_kernel(tc, query, key, value, out):
             side_by_side = bank[:].rearrange("p g u q -> p g (u q)").rearrange("p g (q u) -> p g q u", u=2)
             for a in range(4):
                 c = 4 * half + a
-                out = side_by_side[:, a // 2, :, a % 2] if i >= LAST - 2 else bank[:, a // 2, a % 2, :]
+                out = side_by_side[:, a // 2, :, a % 2] if by_vector(i, half) else bank[:, a // 2, a % 2, :]
                 nc.tensor.transpose(out, words[:, c * P : (c + 1) * P], ident_words[:])
 
         def planes_out(i, half):
@@ -264,7 +267,7 @@ def tile_dotattention_kernel(tc, query, key, value, out):
             bank = plane_bank[(i, half)]
             start = i % 2 * S + half * HALF
             dst = grouped[i // 2][:, start : start + HALF].bitcast(F32)
-            if i >= LAST - 2:
+            if by_vector(i, half):
                 nc.vector.tensor_copy(out=dst, in_=bank[:].rearrange("p g u q -> p (g u q)"))
             else:
                 nc.scalar.copy(
@@ -290,7 +293,10 @@ def tile_dotattention_kernel(tc, query, key, value, out):
                 return
             h = i // TILES
             if i % GROUP == 0:
-                out_bank[i // GROUP] = ps_o.tile([P, GROUP, D], F32, name="o")
+                if i // GROUP == LAST // GROUP:
+                    out_bank[i // GROUP] = ps_s.tile([P, GROUP, D], F32, name="s")
+                else:
+                    out_bank[i // GROUP] = ps_o.tile([P, GROUP, D], F32, name="o")
             for g in range(PASSES):
                 cols = slice(g * P, (g + 1) * P)
                 e_cols = slice((i % 2 * PASSES + g) * P, (i % 2 * PASSES + g + 1) * P)
@@ -327,33 +333,36 @@ def tile_dotattention_kernel(tc, query, key, value, out):
 
         last = {}
 
-        def last_exponential(half):
-            cols = slice(half * HALF, (half + 1) * HALF)
-            if half == 0:
+        def last_exponential(part):
+            cols = (slice(0, HALF), slice(HALF, HALF + BANK), slice(HALF + BANK, S))[part]
+            if part == 0:
                 e_bf16[LAST] = work.tile([P, S], BF16, name="e")
-                last["sums"] = small.tile([P, 2], F32, name="hs")
+                last["sums"] = small.tile([P, 3], F32, name="hs")
             nc.scalar.activation(
                 out=e_bf16[LAST][:, cols],
                 in_=neg_score[LAST][:, cols],
                 func=ACT.Exp,
                 bias=neg_max[LAST][:, 0:1],
                 scale=-1.0,
-                accum_out=last["sums"][:, half : half + 1],
+                accum_out=last["sums"][:, part : part + 1],
             )
-            if half == 1:
+            if part == 2:
                 nc.gpsimd.tensor_scalar(
                     out=row_sum[LAST // GROUP][:, GROUP - 1 : GROUP],
                     in0=last["sums"][:, 0:1],
                     scalar1=last["sums"][:, 1:2],
-                    scalar2=1.0,
+                    scalar2=last["sums"][:, 2:3],
                     op0=ALU.add,
-                    op1=ALU.mult,
+                    op1=ALU.add,
                 )
 
         def last_transpose(g):
             if g == 0:
                 last["grouped"] = work.tile([P, S], BF16, name="grp", align_bytes=64)
-            bank = ps_s.tile([P, P, 2], F32, name="s")
+            if g < 2:
+                bank = ps_s.tile([P, P, 2], F32, name="s")
+            else:
+                bank = ps_t.tile([P, P, 2], F32, name="tb")
             last[g] = bank
             words = e_bf16[LAST][:].bitcast(F32)
             for u in range(2):
@@ -424,7 +433,7 @@ def tile_dotattention_kernel(tc, query, key, value, out):
         score(0, 1)
         first_query(1, FIRST - 1)
         first_key(3, "scalar")
-        for p in range(-3, LAST - 1):
+        for p in range(-3, LAST - 2):
             h, n = divmod(p, TILES)
             ahead = 0 <= h < H - 1
             score(p + 3, 2)
@@ -439,9 +448,7 @@ def tile_dotattention_kernel(tc, query, key, value, out):
             score_out(p + 3, 1)
             score(p + 4, 1)
             exponential(p + 1)
-            if p == LAST - 2:
-                quantise_e(p - 1, 1)
-            elif p % 2 == 0:
+            if p % 2 == 0:
                 quantise_e(p - 2, 2)
             key_out()
             if p == 1:
@@ -471,9 +478,18 @@ def tile_dotattention_kernel(tc, query, key, value, out):
                 first_query(FIRST + 8, TILES - FIRST - 8)
             if ahead and n % 2 == 1 and n < 8 and (h > 0 or n > 1):
                 transpose_half(h + 1, "key" if n < 4 else "query", (n // 2) % 2)
+        e_times_value(LAST - 5)
+        e_times_value(LAST - 4)
+        exponential(LAST - 1)
+        planes_out(LAST - 2, 0)
+        planes_out(LAST - 2, 1)
+        quantise_e(LAST - 3, 1)
+        transpose_e(LAST - 1, 0)
+        transpose_e(LAST - 1, 1)
         e_times_value(LAST - 3)
         last_exponential(0)
         last_exponential(1)
+        last_exponential(2)
         quantise_e(LAST - 2, 1)
         planes_out(LAST - 1, 0)
         last_transpose(0)
@@ -487,10 +503,11 @@ def tile_dotattention_kernel(tc, query, key, value, out):
         last_transpose(2)
         last_transpose(3)
         e_times_value(LAST - 1)
-        last_planes_out(2, "vector")
+        last_planes_out(2, "scalar")
         last_planes_out(3, "scalar")
         last_invert()
         last_quantise(1)
+        normalise_and_store(LAST - 4)
         for g in range(PASSES):
             last_e_times_value(g)
         last_group_out()

@@ -132,7 +132,11 @@ def tile_dotattention_kernel(tc, query, key, value, out):
                     continue
                 if name == "query":
                     cols = slice(half * HALF, (half + 1) * HALF)
-                    nc.scalar.copy(out=qT[h][:, cols], in_=bank[:].rearrange("p a b c -> p (a b c)"))
+                    columns = bank[:].rearrange("p a b c -> p (a b c)")
+                    if h == H - 1:
+                        nc.vector.tensor_copy(out=qT[h][:, cols], in_=columns)
+                    else:
+                        nc.scalar.copy(out=qT[h][:, cols], in_=columns)
                     continue
                 staged = work.tile([P, 2, PACK, P], BF16, name="ks")
                 if h >= 2:

from contextlib import ExitStack

import concourse.mybir as mybir
from concourse.masks import make_identity

F32 = mybir.dt.float32
BF16 = mybir.dt.bfloat16
U32 = mybir.dt.uint32
U8 = mybir.dt.uint8
FP8X4 = mybir.dt.float8_e4m3fn_x4
AX = mybir.AxisListType
ALU = mybir.AluOpType
ACT = mybir.ActivationFunctionType

P = 128
PACK = 4
H = 4
S = 2048
D = 128
TILES = S // P
PASSES = S // (P * PACK)
BANK = 512
HALF = S // 2
GROUP = 4
NT = H * TILES
LAST = NT - 1
FIRST = 4
WARM_UP = 12
FLOPS = 2 * 2 * H * S * S * D


def tile_dotattention_kernel(tc, query, key, value, out):
    nc = tc.nc
    with ExitStack() as ctx:
        const = ctx.enter_context(tc.tile_pool(name="const", bufs=1))
        raw = ctx.enter_context(tc.tile_pool(name="raw", bufs=H))
        keep = ctx.enter_context(tc.tile_pool(name="keep", bufs=2))
        work = ctx.enter_context(tc.tile_pool(name="work", bufs=3))
        deep = ctx.enter_context(tc.tile_pool(name="deep", bufs=4))
        small = ctx.enter_context(tc.tile_pool(name="small", bufs=4))
        ps_s = ctx.enter_context(tc.psum_pool(name="ps_s", bufs=PASSES))
        ps_t = ctx.enter_context(tc.psum_pool(name="ps_t", bufs=3))
        ps_o = ctx.enter_context(tc.psum_pool(name="ps_o", bufs=1))
        ctx.enter_context(tc.manual_schedule())

        q_raw, k_raw, v_raw = [], [], []

        def load_value(h):
            vr = raw.tile([P, PASSES, PACK, D], BF16, name="vr")
            nc.sync.dma_start(out=vr[:], in_=value[0, h].rearrange("(g p t) d -> p g t d", g=PASSES, t=PACK))
            v_raw.append(vr)

        for h in range(H):
            kr = raw.tile([P, PASSES, PACK, D], BF16, name="kr")
            k_view = key[0, h].rearrange("(g p t) d -> p g t d", g=PASSES, t=PACK)
            qr = raw.tile([P, TILES * D], BF16, name="qr")
            q_view = query[0, h].rearrange("(p n) d -> p (n d)", n=TILES)
            if h == 0:
                nc.sync.dma_start(out=kr[:, 0:1], in_=k_view[:, 0:1])
                nc.sync.dma_start(out=qr[:, : FIRST * D], in_=q_view[:, : FIRST * D])
                for g in range(1, PASSES):
                    nc.sync.dma_start(out=kr[:, g : g + 1], in_=k_view[:, g : g + 1])
                nc.sync.dma_start(out=qr[:, FIRST * D :], in_=q_view[:, FIRST * D :])
            else:
                nc.sync.dma_start(out=kr[:], in_=k_view)
                if h == 1:
                    load_value(0)
                nc.sync.dma_start(out=qr[:], in_=q_view)
                load_value(h)
            k_raw.append(kr)
            q_raw.append(qr)

        ident = const.tile([P, P], BF16)
        make_identity(nc, ident[:])
        ident_words = const.tile([P, P], F32)
        make_identity(nc, ident_words[:])
        warm = const.tile([P, 1], F32)
        nc.vector.memset(warm[:], 0.0)
        nc.scalar.activation(out=warm[:], in_=warm[:], func=ACT.Exp)

        minus_one = const.tile([P, GROUP], F32)
        nc.gpsimd.memset(minus_one[:], -1.0)
        zeros = const.tile([P, P], BF16)
        nc.vector.memset(zeros[:], 0.0)
        unread = ps_t.tile([P, P], F32, name="tb")
        for step in range(WARM_UP):
            nc.tensor.matmul(out=unread[:], lhsT=zeros[:], rhs=zeros[:], start=True, stop=True)

        kT, qT, v_grouped, v_codes, v_scales = {}, {}, {}, {}, {}
        waiting, unordered = [], []

        def transpose_half(h, name, half):
            if h not in kT:
                kT[h] = keep.tile([P, S], BF16, name="kt")
                qT[h] = keep.tile([P, S], BF16, name="qt")
            bank = ps_t.tile([P, 2, PACK, P], BF16, name="tb")
            for a in range(2 * PACK):
                if name == "key":
                    rows = k_raw[h][:, 2 * half + a // PACK, a % PACK, :]
                else:
                    n = 2 * PACK * half + a
                    rows = q_raw[h][:, n * D : (n + 1) * D]
                nc.tensor.transpose(bank[:, a // PACK, a % PACK, :], rows, ident[:])
            waiting.append((h, name, half, bank))

        def first_key(g, engine):
            bank = ps_t.tile([P, PACK, P], BF16, name="tb")
            for t in range(PACK):
                nc.tensor.transpose(bank[:, t, :], k_raw[0][:, g, t, :], ident[:])
            stepped = bank[:].rearrange("d (u e) p -> d u p e", u=2)
            if engine == "vector":
                nc.vector.tensor_copy(out=key_columns(0, g), in_=stepped)
            else:
                nc.scalar.copy(out=key_columns(0, g), in_=stepped)

        def first_query(n0, count):
            bank = ps_t.tile([P, count, P], BF16, name="tb")
            for a in range(count):
                nc.tensor.transpose(bank[:, a, :], q_raw[0][:, (n0 + a) * D : (n0 + a + 1) * D], ident[:])
            if n0 + count == TILES:
                waiting.append((0, "first query", n0, bank))
                return
            nc.scalar.copy(out=qT[0][:, n0 * P : (n0 + count) * P], in_=bank[:].rearrange("p a c -> p (a c)"))

        def key_columns(h, g):
            return kT[h][:, g * BANK : (g + 1) * BANK].rearrange("d (u p e) -> d u p e", u=2, e=2)

        def key_out():
            for h, name, half, bank in waiting:
                if name == "first query":
                    nc.scalar.copy(out=qT[h][:, half * P :], in_=bank[:].rearrange("p a c -> p (a c)"))
                    continue
                if name == "query":
                    cols = slice(half * HALF, (half + 1) * HALF)
                    columns = bank[:].rearrange("p a b c -> p (a b c)")
                    if h == H - 1:
                        nc.vector.tensor_copy(out=qT[h][:, cols], in_=columns)
                    else:
                        nc.scalar.copy(out=qT[h][:, cols], in_=columns)
                    continue
                staged = work.tile([P, 2, PACK, P], BF16, name="ks")
                if h >= 2:
                    nc.vector.tensor_copy(out=staged[:], in_=bank[:])
                else:
                    nc.scalar.copy(out=staged[:], in_=bank[:])
                unordered.extend((h, 2 * half + a, staged) for a in range(2))
            waiting.clear()

        def order_key():
            if unordered:
                h, g, staged = unordered[0]
                unordered.remove(unordered[0])
                nc.gpsimd.tensor_scalar(
                    out=key_columns(h, g),
                    in0=staged[:, g % 2].rearrange("d (u e) p -> d u p e", u=2),
                    scalar1=1.0,
                    scalar2=0.0,
                    op0=ALU.mult,
                    op1=ALU.add,
                )

        def group_value(h, g):
            if g == 0:
                v_grouped[h] = keep.tile([P, PASSES, D, PACK], BF16, name="vg", align_bytes=64)
            nc.gpsimd.tensor_scalar(
                out=v_grouped[h][:, g],
                in0=v_raw[h][:, g].rearrange("p t d -> p d t"),
                scalar1=1.0,
                scalar2=0.0,
                op0=ALU.mult,
                op1=ALU.add,
            )

        def quantise_value(h):
            v_codes[h] = keep.tile([P, PASSES * D], U32, name="vc", align_bytes=64)
            v_scales[h] = keep.tile([P, PASSES * D], U8, name="vs", align_bytes=64)
            nc.vector.quantize_mx(
                out=v_codes[h][:].bitcast(FP8X4),
                scales=v_scales[h][:],
                in_=v_grouped[h][:].rearrange("p g d t -> p (g d t)"),
            )

        score_bank, neg_score, bank_min, neg_max, row_sum, e_bf16 = {}, {}, {}, {}, {}, {}
        plane_bank, inverse, grouped, e_codes, e_scales, out_bank = {}, {}, {}, {}, {}, {}

        def live(i):
            return 0 <= i < NT

        def by_vector(i, half):
            return 2 * i + half >= 2 * (LAST - 3) + 1

        def score(i, j):
            if not live(i):
                return
            h, n = divmod(i, TILES)
            score_bank[(i, j)] = ps_s.tile([P, BANK], F32, name="s")
            nc.tensor.matmul(
                out=score_bank[(i, j)][:],
                lhsT=qT[h][:, n * P : (n + 1) * P],
                rhs=kT[h][:, j * BANK : (j + 1) * BANK],
                start=True,
                stop=True,
            )

        def score_out(i, j):
            if not live(i):
                return
            if j == 0:
                bank_min[i] = small.tile([P, PASSES], F32, name="mn")
                neg_score[i] = deep.tile([P, S], F32, name="sb")
            nc.vector.tensor_scalar(
                out=neg_score[i][:, j * BANK : (j + 1) * BANK],
                in0=score_bank[(i, j)][:],
                scalar1=-1.0 / D,
                scalar2=None,
                op0=ALU.mult,
                op1=ALU.min,
                accum_out=bank_min[i][:, j : j + 1],
            )
            if j == PASSES - 1:
                first_three = small.tile([P, 1], F32, name="m3")
                nc.gpsimd.tensor_scalar(
                    out=first_three[:],
                    in0=bank_min[i][:, 0:1],
                    scalar1=bank_min[i][:, 1:2],
                    scalar2=bank_min[i][:, 2:3],
                    op0=ALU.min,
                    op1=ALU.min,
                )
                neg_max[i] = small.tile([P, 1], F32, name="nm")
                nc.gpsimd.tensor_scalar(
                    out=neg_max[i][:],
                    in0=first_three[:],
                    scalar1=bank_min[i][:, 3:4],
                    scalar2=None,
                    op0=ALU.min,
                )

        def exponential(i):
            if not live(i):
                return
            if i % GROUP == 0:
                row_sum[i // GROUP] = small.tile([P, GROUP], F32, name="rs")
            e_bf16[i] = work.tile([P, S], BF16, name="e")
            nc.scalar.activation(
                out=e_bf16[i][:],
                in_=neg_score[i][:],
                func=ACT.Exp,
                bias=neg_max[i][:, 0:1],
                scale=-1.0,
                accum_out=row_sum[i // GROUP][:, i % GROUP : i % GROUP + 1],
            )

        def transpose_e(i, half):
            if not live(i):
                return
            bank = ps_t.tile([P, 2, 2, P], F32, name="tb")
            plane_bank[(i, half)] = bank
            if half == 0 and i % 2 == 0:
                grouped[i // 2] = work.tile([P, 2 * S], BF16, name="grp", align_bytes=64)
            words = e_bf16[i][:].bitcast(F32)
            side_by_side = bank[:].rearrange("p g u q -> p g (u q)").rearrange("p g (q u) -> p g q u", u=2)
            for a in range(4):
                c = 4 * half + a
                out = side_by_side[:, a // 2, :, a % 2] if by_vector(i, half) else bank[:, a // 2, a % 2, :]
                nc.tensor.transpose(out, words[:, c * P : (c + 1) * P], ident_words[:])

        def planes_out(i, half):
            if not live(i):
                return
            bank = plane_bank[(i, half)]
            start = i % 2 * S + half * HALF
            dst = grouped[i // 2][:, start : start + HALF].bitcast(F32)
            if by_vector(i, half):
                nc.vector.tensor_copy(out=dst, in_=bank[:].rearrange("p g u q -> p (g u q)"))
            else:
                nc.scalar.copy(
                    out=dst.rearrange("p (g q u) -> p g q u", g=2, u=2), in_=bank[:].rearrange("p g u q -> p g q u")
                )

        def quantise_e(i, tiles):
            if not live(i):
                return
            pair, place = divmod(i, 2)
            if place == 0:
                e_codes[pair] = work.tile([P, 2 * PASSES * P], U32, name="ec", align_bytes=64)
                e_scales[pair] = work.tile([P, 2 * PASSES * P], U8, name="es", align_bytes=64)
            words = slice(place * PASSES * P, (place + tiles) * PASSES * P)
            nc.vector.quantize_mx(
                out=e_codes[pair][:, words].bitcast(FP8X4),
                scales=e_scales[pair][:, words],
                in_=grouped[pair][:, place * S : (place + tiles) * S],
            )

        def e_times_value(i):
            if not live(i):
                return
            h = i // TILES
            if i % GROUP == 0:
                if i // GROUP == LAST // GROUP:
                    out_bank[i // GROUP] = ps_s.tile([P, GROUP, D], F32, name="s")
                else:
                    out_bank[i // GROUP] = ps_o.tile([P, GROUP, D], F32, name="o")
            for g in range(PASSES):
                cols = slice(g * P, (g + 1) * P)
                e_cols = slice((i % 2 * PASSES + g) * P, (i % 2 * PASSES + g + 1) * P)
                nc.tensor.matmul_mx(
                    out=out_bank[i // GROUP][:, i % GROUP, :],
                    lhsT=e_codes[i // 2][:, e_cols].bitcast(FP8X4),
                    lhsT_scale=e_scales[i // 2][:, e_cols],
                    rhs=v_codes[h][:, cols].bitcast(FP8X4),
                    rhs_scale=v_scales[h][:, cols],
                    start=(g == 0),
                    stop=(g == PASSES - 1),
                )

        def invert_sums(group):
            inverse[group] = small.tile([P, GROUP], F32, name="rc")
            nc.gpsimd.tensor_tensor(
                out=inverse[group][:], in0=row_sum[group][:], in1=minus_one[:], op=ALU.pow
            )

        def normalise_and_store(i):
            if not live(i) or i % GROUP != GROUP - 1:
                return
            h, n = divmod(i, TILES)
            result = small.tile([P, GROUP, D], F32, name="ob")
            nc.vector.tensor_tensor(
                out=result[:],
                in0=out_bank[i // GROUP][:],
                in1=inverse[i // GROUP][:].unsqueeze(2).to_broadcast([P, GROUP, D]),
                op=ALU.mult,
            )
            nc.sync.dma_start(
                out=out[0, h].rearrange("(p n) d -> p n d", n=TILES)[:, n - GROUP + 1 : n + 1, :], in_=result[:]
            )

        last = {}

        def last_exponential(part):
            cols = (slice(0, HALF), slice(HALF, HALF + BANK), slice(HALF + BANK, S))[part]
            if part == 0:
                e_bf16[LAST] = work.tile([P, S], BF16, name="e")
                last["sums"] = small.tile([P, 3], F32, name="hs")
            nc.scalar.activation(
                out=e_bf16[LAST][:, cols],
                in_=neg_score[LAST][:, cols],
                func=ACT.Exp,
                bias=neg_max[LAST][:, 0:1],
                scale=-1.0,
                accum_out=last["sums"][:, part : part + 1],
            )
            if part == 2:
                nc.gpsimd.tensor_scalar(
                    out=row_sum[LAST // GROUP][:, GROUP - 1 : GROUP],
                    in0=last["sums"][:, 0:1],
                    scalar1=last["sums"][:, 1:2],
                    scalar2=last["sums"][:, 2:3],
                    op0=ALU.add,
                    op1=ALU.add,
                )

        def last_transpose(g):
            if g == 0:
                last["grouped"] = work.tile([P, S], BF16, name="grp", align_bytes=64)
            if g < 2:
                bank = ps_s.tile([P, P, 2], F32, name="s")
            else:
                bank = ps_t.tile([P, P, 2], F32, name="tb")
            last[g] = bank
            words = e_bf16[LAST][:].bitcast(F32)
            for u in range(2):
                c = 2 * g + u
                nc.tensor.transpose(bank[:, :, u], words[:, c * P : (c + 1) * P], ident_words[:])

        def last_planes_out(g, engine):
            dst = last["grouped"][:, g * BANK : (g + 1) * BANK].bitcast(F32)
            src = last[g][:].rearrange("p q u -> p (q u)")
            if engine == "vector":
                nc.vector.tensor_copy(out=dst, in_=src)
            else:
                nc.scalar.copy(out=dst, in_=src)

        def last_quantise(half):
            if half == 0:
                last["codes"] = work.tile([P, PASSES * P], U32, name="ec", align_bytes=64)
                last["scales"] = work.tile([P, PASSES * P], U8, name="es", align_bytes=64)
            cols = slice(half * 2 * P, (half + 1) * 2 * P)
            nc.vector.quantize_mx(
                out=last["codes"][:, cols].bitcast(FP8X4),
                scales=last["scales"][:, cols],
                in_=last["grouped"][:, half * HALF : (half + 1) * HALF],
            )

        def last_e_times_value(g):
            if g == 0:
                last["out"] = ps_s.tile([P, D], F32, name="s")
            cols = slice(g * P, (g + 1) * P)
            nc.tensor.matmul_mx(
                out=last["out"][:],
                lhsT=last["codes"][:, cols].bitcast(FP8X4),
                lhsT_scale=last["scales"][:, cols],
                rhs=v_codes[H - 1][:, cols].bitcast(FP8X4),
                rhs_scale=v_scales[H - 1][:, cols],
                start=(g == 0),
                stop=(g == PASSES - 1),
            )

        def last_invert():
            last["inverse"] = small.tile([P, GROUP], F32, name="rc")
            nc.vector.reciprocal(out=last["inverse"][:], in_=row_sum[LAST // GROUP][:])

        def last_group_out():
            view = out[0, H - 1].rearrange("(p n) d -> p n d", n=TILES)
            last_inverse = last["inverse"]
            three = small.tile([P, GROUP - 1, D], F32, name="ob")
            nc.vector.tensor_tensor(
                out=three[:],
                in0=out_bank[LAST // GROUP][:, : GROUP - 1, :],
                in1=last_inverse[:, : GROUP - 1].unsqueeze(2).to_broadcast([P, GROUP - 1, D]),
                op=ALU.mult,
            )
            nc.sync.dma_start(out=view[:, TILES - GROUP : TILES - 1, :], in_=three[:])
            one = small.tile([P, D], F32, name="ol")
            nc.vector.tensor_scalar(
                out=one[:], in0=last["out"][:], scalar1=last_inverse[:, GROUP - 1 : GROUP], scalar2=None, op0=ALU.mult
            )
            nc.sync.dma_start(out=view[:, TILES - 1, :], in_=one[:])

        kT[0] = keep.tile([P, S], BF16, name="kt")
        qT[0] = keep.tile([P, S], BF16, name="qt")
        first_key(0, "vector")
        first_query(0, 1)
        first_key(1, "vector")
        score(0, 0)
        first_key(2, "scalar")
        score(0, 1)
        first_query(1, FIRST - 1)
        first_key(3, "scalar")
        for p in range(-3, LAST - 2):
            h, n = divmod(p, TILES)
            ahead = 0 <= h < H - 1
            score(p + 3, 2)
            score(p + 3, 3)
            if p == -3:
                first_query(FIRST, 8)
            if p % 2 == 1:
                e_times_value(p - 3)
                e_times_value(p - 2)
            score_out(p + 3, 0)
            score(p + 4, 0)
            score_out(p + 3, 1)
            score(p + 4, 1)
            exponential(p + 1)
            if p % 2 == 0:
                quantise_e(p - 2, 2)
            key_out()
            if p == 1:
                quantise_value(0)
            if ahead and n == 12:
                quantise_value(h + 1)
            planes_out(p, 0)
            if p in (-2, -1):
                group_value(0, 2 * (p + 2))
                group_value(0, 2 * (p + 2) + 1)
            if ahead and 8 <= n < 8 + PASSES:
                group_value(h + 1, n - 8)
            transpose_e(p + 1, 0)
            score_out(p + 3, 2)
            score_out(p + 3, 3)
            if p >= 0:
                order_key()
            if p >= 0 and p % GROUP == GROUP - 1:
                invert_sums(p // GROUP)
            planes_out(p, 1)
            transpose_e(p + 1, 1)
            normalise_and_store(p - 2)
            if p == -3:
                transpose_half(1, "key", 0)
                key_out()
            if p == 0:
                first_query(FIRST + 8, TILES - FIRST - 8)
            if ahead and n % 2 == 1 and n < 8 and (h > 0 or n > 1):
                transpose_half(h + 1, "key" if n < 4 else "query", (n // 2) % 2)
        e_times_value(LAST - 5)
        e_times_value(LAST - 4)
        exponential(LAST - 1)
        planes_out(LAST - 2, 0)
        planes_out(LAST - 2, 1)
        quantise_e(LAST - 3, 1)
        transpose_e(LAST - 1, 0)
        transpose_e(LAST - 1, 1)
        e_times_value(LAST - 3)
        last_exponential(0)
        last_exponential(1)
        last_exponential(2)
        quantise_e(LAST - 2, 1)
        planes_out(LAST - 1, 0)
        last_transpose(0)
        last_transpose(1)
        planes_out(LAST - 1, 1)
        e_times_value(LAST - 2)
        last_planes_out(0, "vector")
        last_planes_out(1, "vector")
        quantise_e(LAST - 1, 1)
        last_quantise(0)
        last_transpose(2)
        last_transpose(3)
        e_times_value(LAST - 1)
        last_planes_out(2, "scalar")
        last_planes_out(3, "scalar")
        last_invert()
        last_quantise(1)
        normalise_and_store(LAST - 4)
        for g in range(PASSES):
            last_e_times_value(g)
        last_group_out()
